import numpy as np
import ml_dtypes


def mxq(x, axis, fmt="e4m3"):
    dtype, down = {"e4m3": (ml_dtypes.float8_e4m3fn, 7), "e5m2": (ml_dtypes.float8_e5m2, 14)}[fmt]
    v = np.moveaxis(np.asarray(x, np.float32).astype(ml_dtypes.bfloat16).astype(np.float64), axis, -1)
    blocks = v.reshape(v.shape[:-1] + (-1, 32))
    amax = np.abs(blocks).max(-1, keepdims=True)
    byte = np.maximum(np.where(amax > 0, np.frexp(amax)[1] - 1 + 127, 0) - down, 1)
    scale = np.exp2(byte - 127.0)
    codes = (blocks / scale).astype(np.float32).astype(dtype).astype(np.float64)
    return np.moveaxis((codes * scale).reshape(v.shape), -1, axis)


WIDE = False


def mx_kscale(k):
    if not WIDE:
        return np.ones(k)
    levels = np.array([10, -10, 5, -5, 0])
    if k % 512:
        return np.exp2(np.random.permutation(np.resize(levels, k // 32))).repeat(32)
    a = np.empty((k // 512, 16))
    for p in range(k // 512):
        a[p, :8] = np.random.permutation(np.resize(levels, 8))
        for g in range(8):
            far = levels[np.abs(levels - a[p, g]) >= 10]
            a[p, g + 8] = far[np.random.randint(len(far))]
    return np.exp2(a.ravel()).repeat(32)


BF16 = ml_dtypes.bfloat16


def bf(x):
    return np.asarray(x, np.float32).astype(BF16)


def f64(x):
    return np.asarray(x).astype(np.float64)


B, D, S, N = 4096, 1024, 2, 128
DS = D // S


def sigmoid(v):
    return 1.0 / (1.0 + np.exp(-v))


def setup_inputs():
    s = mx_kscale(D)
    t = np.maximum(1.0 + 2.0 * np.random.standard_normal((B, N, S)), 0.0) + np.maximum(1.0 + 2.0 * np.random.standard_normal((B, N, S)), 0.0)
    return {"a": bf(t * t / (t * t).sum(axis=1, keepdims=True)),
            "vr": bf(np.random.standard_normal((N, S, DS)) * 0.5 * np.sqrt(N) * s.reshape(S, DS)),
            "h": bf(np.random.standard_normal((B, D)) * s),
            "x2g": bf(np.random.standard_normal((B, D))),
            "w_g": bf(np.random.standard_normal((D, D)) / np.sqrt(D) / s),
            "b_g": bf(np.random.standard_normal(D) * 0.3),
            "bg": bf(1.0 + 0.1 * np.random.standard_normal(1))}


def reference(a, vr, h, x2g, w_g, b_g, bg):
    hf = f64(h)
    hh = (f64(a).transpose(2, 0, 1) @ f64(vr).transpose(1, 0, 2)).transpose(1, 0, 2).reshape(B, D)
    h2g = (mxq(hf, 1, "e4m3") @ mxq(f64(w_g), 1, "e4m3").T) + f64(b_g)
    g = sigmoid(f64(x2g) + h2g + f64(bg))
    return g * hh + (1.0 - g) * hf

@@ -1,0 +1,315 @@
+from contextlib import ExitStack
+
+import concourse.mybir as mybir
+from concourse.masks import make_identity
+
+F32 = mybir.dt.float32
+BF16 = mybir.dt.bfloat16
+U32 = mybir.dt.uint32
+U8 = mybir.dt.uint8
+FP8X4 = mybir.dt.float8_e4m3fn_x4
+ALU = mybir.AluOpType
+ACT = mybir.ActivationFunctionType
+
+P = 128
+B, D, S, N = 4096, 1024, 2, 128
+DS = D // S
+ROWS = 4
+GROUPS = B // (P * ROWS)
+NT = GROUPS * ROWS
+K0 = 6
+TF = 5
+
+FLOPS = 2 * B * D * D + 2 * B * N * D
+
+
+def word_step(blk):
+    g, u = divmod(blk, 2)
+    return slice(256 * g + u, 256 * g + 256, 2)
+
+
+def is_x(r):
+    return r % 2 == 0
+
+
+def p0_on_gpsimd(r):
+    return r >= 6 and r % 3 == 0
+
+
+def tile_tpru_pb_t_kernel(tc, a, vr, h, x2g, w_g, b_g, bg, out):
+    nc = tc.nc
+    h_v = h.rearrange("(q p i) k -> q p i k", p=P, i=ROWS)
+    x_v = x2g.rearrange("(q p i) k -> q p i k", p=P, i=ROWS)
+    a_v = a.rearrange("(q p i) n s -> q p i (n s)", p=P, i=ROWS)
+    o_v = out.rearrange("(q p i) k -> q p i k", p=P, i=ROWS)
+    w_v = w_g.rearrange("(j p) k -> p j k", p=P)
+
+    with ExitStack() as ctx:
+        const = ctx.enter_context(tc.tile_pool(name="const", bufs=1))
+        ld = ctx.enter_context(tc.tile_pool(name="ld", bufs=3))
+        work = ctx.enter_context(tc.tile_pool(name="work", bufs=2))
+        psum = ctx.enter_context(tc.psum_pool(name="psum", bufs=2))
+        psb = ctx.enter_context(tc.psum_pool(name="psb", bufs=1))
+
+        h_sb, x_sb, a_sb, aT_sb, tp_ps, ta_ps = {}, {}, {}, {}, {}, {}
+        hg_sb, hc_sb, hs_sb, nh_sb, acc_ps, hh_ps, z_sb, o_sb = {}, {}, {}, {}, {}, {}, {}, {}
+
+        def load_x(q):
+            x_sb[q] = ld.tile([P, ROWS, D], BF16, name="x_t", tag="x")
+            nc.sync.dma_start(out=x_sb[q][:], in_=x_v[q])
+
+        def load_h(q):
+            h_sb[q] = ld.tile([P, ROWS, D], BF16, name="h_t", tag="h", bufs=4)
+            nc.sync.dma_start(out=h_sb[q][:], in_=h_v[q])
+
+        def load_a(q):
+            a_sb[q] = ld.tile([P, ROWS, 2 * N], BF16, name="a_t", tag="a")
+            nc.sync.dma_start(out=a_sb[q][:], in_=a_v[q])
+
+        ident_f = const.tile([P, P], F32, name="ident_f")
+        make_identity(nc, ident_f[:])
+        ident_b = const.tile([P, P], BF16, name="ident_b")
+        make_identity(nc, ident_b[:])
+        neg_i = const.tile([P, P], BF16, name="neg_i")
+        nc.vector.tensor_scalar_mul(out=neg_i[:], in0=ident_b[:], scalar1=-1.0)
+
+        brow = const.tile([P, P], BF16, name="brow")
+        nc.vector.memset(brow[:], 0.0)
+        nc.sync.dma_start(out=brow[0:8, :], in_=b_g.rearrange("(j c) -> j c", c=P))
+        bg_b = const.tile([P, 1], BF16, name="bg_b")
+        nc.sync.dma_start(out=bg_b[:], in_=bg.partition_broadcast(P))
+
+        wc = const.tile([P, 2, D], U32, name="wc", align_bytes=64)
+        ws = const.tile([P, 2, D], U8, name="ws", align_bytes=64)
+        vr_sb = const.tile([P, S, DS], BF16, name="vr_sb")
+        vrp_sb = const.tile([P, S, DS], BF16, name="vrp_sb")
+        bias_sb = const.tile([P, D], F32, name="bias_sb")
+
+        wtmp = tc.tile_pool(name="wtmp", bufs=1)
+        with wtmp as wt:
+            load_x(0)
+            wraw = wt.tile([P, 8, D], BF16, name="wraw")
+            nc.sync.dma_start(out=wraw[:, 0:4, :], in_=w_v[:, 0:4, :])
+            h_sb[0] = ld.tile([P, ROWS, D], BF16, name="h_t", tag="h", bufs=4)
+            nc.sync.dma_start(out=h_sb[0][:, 0:1, :], in_=h_v[0][:, 0:1, :])
+            nc.sync.dma_start(out=wraw[:, 4:8, :], in_=w_v[:, 4:8, :])
+            load_a(0)
+            nc.sync.dma_start(out=vr_sb[:], in_=vr)
+            nc.sync.dma_start(out=h_sb[0][:, 1:4, :], in_=h_v[0][:, 1:4, :])
+            load_x(1)
+            load_h(1)
+            load_a(1)
+
+            nc.vector.tensor_copy(
+                out=vrp_sb[:].rearrange("n s (t p) -> n s t p", t=4, p=P),
+                in_=vr_sb[:].rearrange("n s (p t) -> n s t p", t=4, p=P),
+            )
+
+            b_t = psum.tile([P, P], BF16, name="b_t", tag="tp")
+            nc.tensor.transpose(b_t[:], brow[:], ident_b[:])
+            bg_f = const.tile([P, 1], F32, name="bg_f")
+            nc.vector.tensor_copy(out=bg_f[:], in_=bg_b[:])
+            bcol = const.tile([P, 8], F32, name="bcol")
+            nc.vector.tensor_scalar_add(out=bcol[:], in0=b_t[:, 0:8], scalar1=bg_f[:, 0:1])
+            brep = wt.tile([P, 8, P], F32, name="brep")
+            nc.vector.tensor_copy(out=brep[:], in_=bcol[:].unsqueeze(2).to_broadcast([P, 8, P]))
+            bias_ps = []
+            for u in range(2):
+                bias_ps.append(psb.tile([P, DS], F32, name="bias%d" % u))
+            for j in range(8):
+                nc.tensor.transpose(bias_ps[j // 4][:, P * (j % 4) : P * (j % 4) + P], brep[:, j, :], ident_f[:])
+            for u in range(2):
+                nc.scalar.copy(out=bias_sb[:, DS * u : DS * u + DS], in_=bias_ps[u][:])
+
+            wg = wt.tile([P, 2 * D * 4], BF16, name="wg", align_bytes=64)
+            wg_f = wg[:].bitcast(F32).rearrange("p (g c u) -> p g c u", g=2, c=D, u=2)
+            wg_q = wg[:].rearrange("p (g x) -> p g x", g=2)
+            for j in range(8):
+                tpw = psum.tile([P, 4, P], F32, name="tpw", tag="tp")
+                wj = wraw[:, j, :].bitcast(F32)
+                for blk in range(4):
+                    nc.tensor.transpose(tpw[:, blk, :], wj[:, word_step(blk)], ident_f[:])
+                nc.scalar.copy(
+                    out=wg_f[:, :, P * j : P * j + P, :],
+                    in_=tpw[:].rearrange("p (g u) r -> p g r u", g=2, u=2),
+                )
+                if j % 4 == 3:
+                    u = j // 4
+                    for g in range(2):
+                        nc.vector.quantize_mx(
+                            out=wc[:, g, DS * u : DS * u + DS].bitcast(FP8X4),
+                            scales=ws[:, g, DS * u : DS * u + DS],
+                            in_=wg_q[:, g, 4 * DS * u : 4 * DS * u + 4 * DS],
+                        )
+
+        late = ctx.enter_context(tc.tile_pool(name="late", bufs=3))
+
+        def t_h(r):
+            q, i = divmod(r, ROWS)
+            tp_ps[r] = psum.tile([P, 4, P], F32, name="tph", tag="tp")
+            hw = h_sb[q][:, i, :].bitcast(F32)
+            for blk in range(4):
+                nc.tensor.transpose(tp_ps[r][:, blk, :], hw[:, word_step(blk)], ident_f[:])
+
+        def c_h(r):
+            q, i = divmod(r, ROWS)
+            if i == 0:
+                hg_sb[q] = work.tile([P, ROWS, D], BF16, name="hg", tag="hg", align_bytes=64)
+                hc_sb[q] = work.tile([P, ROWS, 2, P], U32, name="hc", tag="hc", align_bytes=64)
+                hs_sb[q] = work.tile([P, ROWS, 2, P], U8, name="hs", tag="hs", align_bytes=64)
+            nc.scalar.copy(
+                out=hg_sb[q][:, i, :].bitcast(F32).rearrange("p (g r u) -> p g r u", g=2, r=P, u=2),
+                in_=tp_ps[r][:].rearrange("p (g u) r -> p g r u", g=2, u=2),
+            )
+
+        def quant(r0):
+            q, i0 = divmod(r0, ROWS)
+            nc.vector.quantize_mx(
+                out=hc_sb[q][:, i0 : i0 + 2, :, :].rearrange("p i g r -> p (i g r)").bitcast(FP8X4),
+                scales=hs_sb[q][:, i0 : i0 + 2, :, :].rearrange("p i g r -> p (i g r)"),
+                in_=hg_sb[q][:, i0 : i0 + 2, :].rearrange("p i x -> p (i x)"),
+            )
+
+        def nh_make(r):
+            q, i = divmod(r, ROWS)
+            nh_sb[r] = late.tile([P, 2, 4, P], F32, name="nh", tag="nh")
+            for g in range(2):
+                nc.scalar.mul(
+                    out=nh_sb[r][:, g, :, :],
+                    in_=hg_sb[q][:, i, 4 * P * g : 4 * P * g + 4 * P].rearrange("p (r t) -> p t r", r=P, t=4),
+                    mul=-1.0,
+                )
+
+        def t_a(q):
+            ta_ps[q] = psum.tile([P, ROWS, P], F32, name="tpa", tag="tp")
+            for i in range(ROWS):
+                nc.tensor.transpose(ta_ps[q][:, i, :], a_sb[q][:, i, :].bitcast(F32), ident_f[:])
+
+        def c_a(q):
+            aT_sb[q] = work.tile([P, ROWS, S, P], BF16, name="aT", tag="aT")
+            nc.scalar.copy(
+                out=aT_sb[q][:],
+                in_=ta_ps[q][:].rearrange("p i b -> p (i b)").bitcast(BF16).rearrange("p (i b s) -> p i s b", i=ROWS, b=P, s=S),
+            )
+
+        def p0(r):
+            q, i = divmod(r, ROWS)
+            z_sb[r] = work.tile([P, D], F32, name="z_t", tag="z", bufs=K0 + 3)
+            if p0_on_gpsimd(r):
+                nc.gpsimd.tensor_tensor(out=z_sb[r][:], in0=x_sb[q][:, i, :], in1=bias_sb[:], op=ALU.add)
+                return
+            for u in range(2):
+                c = slice(DS * u, DS * u + DS)
+                nc.vector.tensor_tensor(out=z_sb[r][:, c], in0=bias_ps[u][:], in1=x_sb[q][:, i, c], op=ALU.add)
+
+        def mm(r, u):
+            q, i = divmod(r, ROWS)
+            c = slice(DS * u, DS * u + DS)
+            acc = psum.tile([P, DS], F32, name="acc", tag="h2g")
+            for g in range(2):
+                nc.tensor.matmul_mx(
+                    out=acc[:],
+                    lhsT=hc_sb[q][:, i, g, :].bitcast(FP8X4),
+                    lhsT_scale=hs_sb[q][:, i, g, :],
+                    rhs=wc[:, g, c].bitcast(FP8X4),
+                    rhs_scale=ws[:, g, c],
+                    start=(g == 0),
+                    stop=(g == 1),
+                )
+            acc_ps[(r, u)] = acc
+
+        def p1(r, u):
+            c = slice(DS * u, DS * u + DS)
+            nc.vector.tensor_tensor(out=z_sb[r][:, c], in0=acc_ps[(r, u)][:], in1=z_sb[r][:, c], op=ALU.add)
+
+        def d_open(r, s):
+            q, i = divmod(r, ROWS)
+            hb = psum.tile([P, DS], F32, name="hb", tag="hh")
+            rhs = vr_sb if is_x(r) else vrp_sb
+            nc.tensor.matmul(out=hb[:], lhsT=aT_sb[q][:, i, s, :], rhs=rhs[:, s, :], start=True, stop=False)
+            hh_ps[(r, s)] = hb
+
+        def d_close(r, s):
+            q, i = divmod(r, ROWS)
+            hb = hh_ps[(r, s)]
+            if is_x(r):
+                nc.tensor.matmul(out=hb[:], lhsT=neg_i[:], rhs=h_sb[q][:, i, DS * s : DS * s + DS], start=False, stop=True)
+                return
+            for t in range(4):
+                nc.tensor.matmul(
+                    out=hb[:, P * t : P * t + P],
+                    lhsT=nh_sb[r][:, s, t, :],
+                    rhs=ident_f[:],
+                    start=False,
+                    stop=(t == 3),
+                    is_transpose=True,
+                )
+
+        def p4(r, s):
+            c = slice(DS * s, DS * s + DS)
+            if s == 0:
+                o_sb[r] = late.tile([P, D], F32, name="o_t", tag="o", bufs=6)
+            if is_x(r):
+                nc.vector.tensor_tensor(out=o_sb[r][:, c], in0=hh_ps[(r, s)][:], in1=z_sb[r][:, c], op=ALU.mult)
+            else:
+                nc.vector.tensor_tensor(
+                    out=o_sb[r][:, c].rearrange("r (p t) -> r p t", p=P, t=4),
+                    in0=hh_ps[(r, s)][:].rearrange("r (t p) -> r p t", p=P, t=4),
+                    in1=z_sb[r][:, c].rearrange("r (p t) -> r p t", p=P, t=4),
+                    op=ALU.mult,
+                )
+
+        def store(r):
+            q, i = divmod(r, ROWS)
+            nc.sync.dma_start(out=o_v[q][:, i, :], in_=o_sb[r][:])
+
+        def ok(r):
+            return 0 <= r < NT
+
+        with tc.manual_schedule():
+            for r in range(-K0, NT + 3):
+                if r >= -ROWS and r % ROWS == 0 and r // ROWS + 3 < GROUPS:
+                    load_x(r // ROWS + 3)
+                if r >= -1 and r % ROWS == ROWS - 1 and (r + 9) // ROWS < GROUPS:
+                    load_h((r + 9) // ROWS)
+                    load_a((r + 9) // ROWS)
+                for u in range(2):
+                    if ok(r):
+                        p1(r, u)
+                    if ok(r + 1):
+                        mm(r + 1, u)
+                if ok(r):
+                    nc.scalar.activation(out=z_sb[r][:], in_=z_sb[r][:], func=ACT.Sigmoid)
+                if ok(r + 4):
+                    c_h(r + 4)
+                if ok(r - 1):
+                    for s in range(S):
+                        p4(r - 1, s)
+                        if r - 1 == NT - 1:
+                            c = slice(DS * s, DS * s + DS)
+                            nc.vector.tensor_tensor(
+                                out=o_sb[r - 1][:, c], in0=o_sb[r - 1][:, c], in1=h_sb[GROUPS - 1][:, ROWS - 1, c], op=ALU.add
+                            )
+                            nc.sync.dma_start(out=o_v[GROUPS - 1][:, ROWS - 1, c], in_=o_sb[r - 1][:, c])
+                if ok(r):
+                    for s in range(S):
+                        d_open(r, s)
+                    for s in range(S):
+                        d_close(r, s)
+                if (r + 2) % ROWS == 0 and ok(r + 2):
+                    c_a((r + 2) // ROWS)
+                if ok(r + 2) and not is_x(r + 2):
+                    nh_make(r + 2)
+                if ok(r + K0):
+                    p0(r + K0)
+                if ok(r + 2) and (r + 2) % 2 == 0:
+                    quant(r + 2)
+                if ok(r - 1) and r - 1 < NT - 1:
+                    q1, i1 = divmod(r - 1, ROWS)
+                    nc.gpsimd.tensor_tensor(out=o_sb[r - 1][:], in0=o_sb[r - 1][:], in1=h_sb[q1][:, i1, :], op=ALU.add)
+                if ok(r + TF):
+                    t_h(r + TF)
+                if (r + 3) % ROWS == 0 and ok(r + 3):
+                    t_a((r + 3) // ROWS)
+                if ok(r - 2) and r - 2 < NT - 1:
+                    store(r - 2)

@@ -17,8 +17,9 @@ DS = D // S
 ROWS = 4
 GROUPS = B // (P * ROWS)
 NT = GROUPS * ROWS
-K0 = 6
-TF = 5
+K0 = 8
+TF = 7
+CH = 6
 
 FLOPS = 2 * B * D * D + 2 * B * N * D
 
@@ -32,8 +33,8 @@ def is_x(r):
     return r % 2 == 0
 
 
-def p0_on_gpsimd(r):
-    return r >= 6 and r % 3 == 0
+def p0_on_gpsimd(r, u):
+    return r < 8 and r % 2 == 1 or r >= 8 and r % 4 == 1
 
 
 def tile_tpru_pb_t_kernel(tc, a, vr, h, x2g, w_g, b_g, bg, out):
@@ -45,6 +46,7 @@ def tile_tpru_pb_t_kernel(tc, a, vr, h, x2g, w_g, b_g, bg, out):
     w_v = w_g.rearrange("(j p) k -> p j k", p=P)
 
     with ExitStack() as ctx:
+        ctx.enter_context(tc.manual_schedule())
         const = ctx.enter_context(tc.tile_pool(name="const", bufs=1))
         ld = ctx.enter_context(tc.tile_pool(name="ld", bufs=3))
         work = ctx.enter_context(tc.tile_pool(name="work", bufs=2))
@@ -54,95 +56,19 @@ def tile_tpru_pb_t_kernel(tc, a, vr, h, x2g, w_g, b_g, bg, out):
         h_sb, x_sb, a_sb, aT_sb, tp_ps, ta_ps = {}, {}, {}, {}, {}, {}
         hg_sb, hc_sb, hs_sb, nh_sb, acc_ps, hh_ps, z_sb, o_sb = {}, {}, {}, {}, {}, {}, {}, {}
 
-        def load_x(q):
-            x_sb[q] = ld.tile([P, ROWS, D], BF16, name="x_t", tag="x")
-            nc.sync.dma_start(out=x_sb[q][:], in_=x_v[q])
+        def load_x(q, lo=0, hi=ROWS):
+            if lo == 0:
+                x_sb[q] = ld.tile([P, ROWS, D], BF16, name="x_t", tag="x")
+            nc.sync.dma_start(out=x_sb[q][:, lo:hi, :], in_=x_v[q][:, lo:hi, :])
 
-        def load_h(q):
-            h_sb[q] = ld.tile([P, ROWS, D], BF16, name="h_t", tag="h", bufs=4)
-            nc.sync.dma_start(out=h_sb[q][:], in_=h_v[q])
+        def load_h(q, lo=0, hi=ROWS):
+            if lo == 0:
+                h_sb[q] = ld.tile([P, ROWS, D], BF16, name="h_t", tag="h", bufs=4)
+            nc.sync.dma_start(out=h_sb[q][:, lo:hi, :], in_=h_v[q][:, lo:hi, :])
 
         def load_a(q):
             a_sb[q] = ld.tile([P, ROWS, 2 * N], BF16, name="a_t", tag="a")
             nc.sync.dma_start(out=a_sb[q][:], in_=a_v[q])
-
-        ident_f = const.tile([P, P], F32, name="ident_f")
-        make_identity(nc, ident_f[:])
-        ident_b = const.tile([P, P], BF16, name="ident_b")
-        make_identity(nc, ident_b[:])
-        neg_i = const.tile([P, P], BF16, name="neg_i")
-        nc.vector.tensor_scalar_mul(out=neg_i[:], in0=ident_b[:], scalar1=-1.0)
-
-        brow = const.tile([P, P], BF16, name="brow")
-        nc.vector.memset(brow[:], 0.0)
-        nc.sync.dma_start(out=brow[0:8, :], in_=b_g.rearrange("(j c) -> j c", c=P))
-        bg_b = const.tile([P, 1], BF16, name="bg_b")
-        nc.sync.dma_start(out=bg_b[:], in_=bg.partition_broadcast(P))
-
-        wc = const.tile([P, 2, D], U32, name="wc", align_bytes=64)
-        ws = const.tile([P, 2, D], U8, name="ws", align_bytes=64)
-        vr_sb = const.tile([P, S, DS], BF16, name="vr_sb")
-        vrp_sb = const.tile([P, S, DS], BF16, name="vrp_sb")
-        bias_sb = const.tile([P, D], F32, name="bias_sb")
-
-        wtmp = tc.tile_pool(name="wtmp", bufs=1)
-        with wtmp as wt:
-            load_x(0)
-            wraw = wt.tile([P, 8, D], BF16, name="wraw")
-            nc.sync.dma_start(out=wraw[:, 0:4, :], in_=w_v[:, 0:4, :])
-            h_sb[0] = ld.tile([P, ROWS, D], BF16, name="h_t", tag="h", bufs=4)
-            nc.sync.dma_start(out=h_sb[0][:, 0:1, :], in_=h_v[0][:, 0:1, :])
-            nc.sync.dma_start(out=wraw[:, 4:8, :], in_=w_v[:, 4:8, :])
-            load_a(0)
-            nc.sync.dma_start(out=vr_sb[:], in_=vr)
-            nc.sync.dma_start(out=h_sb[0][:, 1:4, :], in_=h_v[0][:, 1:4, :])
-            load_x(1)
-            load_h(1)
-            load_a(1)
-
-            nc.vector.tensor_copy(
-                out=vrp_sb[:].rearrange("n s (t p) -> n s t p", t=4, p=P),
-                in_=vr_sb[:].rearrange("n s (p t) -> n s t p", t=4, p=P),
-            )
-
-            b_t = psum.tile([P, P], BF16, name="b_t", tag="tp")
-            nc.tensor.transpose(b_t[:], brow[:], ident_b[:])
-            bg_f = const.tile([P, 1], F32, name="bg_f")
-            nc.vector.tensor_copy(out=bg_f[:], in_=bg_b[:])
-            bcol = const.tile([P, 8], F32, name="bcol")
-            nc.vector.tensor_scalar_add(out=bcol[:], in0=b_t[:, 0:8], scalar1=bg_f[:, 0:1])
-            brep = wt.tile([P, 8, P], F32, name="brep")
-            nc.vector.tensor_copy(out=brep[:], in_=bcol[:].unsqueeze(2).to_broadcast([P, 8, P]))
-            bias_ps = []
-            for u in range(2):
-                bias_ps.append(psb.tile([P, DS], F32, name="bias%d" % u))
-            for j in range(8):
-                nc.tensor.transpose(bias_ps[j // 4][:, P * (j % 4) : P * (j % 4) + P], brep[:, j, :], ident_f[:])
-            for u in range(2):
-                nc.scalar.copy(out=bias_sb[:, DS * u : DS * u + DS], in_=bias_ps[u][:])
-
-            wg = wt.tile([P, 2 * D * 4], BF16, name="wg", align_bytes=64)
-            wg_f = wg[:].bitcast(F32).rearrange("p (g c u) -> p g c u", g=2, c=D, u=2)
-            wg_q = wg[:].rearrange("p (g x) -> p g x", g=2)
-            for j in range(8):
-                tpw = psum.tile([P, 4, P], F32, name="tpw", tag="tp")
-                wj = wraw[:, j, :].bitcast(F32)
-                for blk in range(4):
-                    nc.tensor.transpose(tpw[:, blk, :], wj[:, word_step(blk)], ident_f[:])
-                nc.scalar.copy(
-                    out=wg_f[:, :, P * j : P * j + P, :],
-                    in_=tpw[:].rearrange("p (g u) r -> p g r u", g=2, u=2),
-                )
-                if j % 4 == 3:
-                    u = j // 4
-                    for g in range(2):
-                        nc.vector.quantize_mx(
-                            out=wc[:, g, DS * u : DS * u + DS].bitcast(FP8X4),
-                            scales=ws[:, g, DS * u : DS * u + DS],
-                            in_=wg_q[:, g, 4 * DS * u : 4 * DS * u + 4 * DS],
-                        )
-
-        late = ctx.enter_context(tc.tile_pool(name="late", bufs=3))
 
         def t_h(r):
             q, i = divmod(r, ROWS)
@@ -162,12 +88,12 @@ def tile_tpru_pb_t_kernel(tc, a, vr, h, x2g, w_g, b_g, bg, out):
                 in_=tp_ps[r][:].rearrange("p (g u) r -> p g r u", g=2, u=2),
             )
 
-        def quant(r0):
+        def quant(r0, nt):
             q, i0 = divmod(r0, ROWS)
             nc.vector.quantize_mx(
-                out=hc_sb[q][:, i0 : i0 + 2, :, :].rearrange("p i g r -> p (i g r)").bitcast(FP8X4),
-                scales=hs_sb[q][:, i0 : i0 + 2, :, :].rearrange("p i g r -> p (i g r)"),
-                in_=hg_sb[q][:, i0 : i0 + 2, :].rearrange("p i x -> p (i x)"),
+                out=hc_sb[q][:, i0 : i0 + nt, :, :].rearrange("p i g r -> p (i g r)").bitcast(FP8X4),
+                scales=hs_sb[q][:, i0 : i0 + nt, :, :].rearrange("p i g r -> p (i g r)"),
+                in_=hg_sb[q][:, i0 : i0 + nt, :].rearrange("p i x -> p (i x)"),
             )
 
         def nh_make(r):
@@ -195,12 +121,12 @@ def tile_tpru_pb_t_kernel(tc, a, vr, h, x2g, w_g, b_g, bg, out):
         def p0(r):
             q, i = divmod(r, ROWS)
             z_sb[r] = work.tile([P, D], F32, name="z_t", tag="z", bufs=K0 + 3)
-            if p0_on_gpsimd(r):
-                nc.gpsimd.tensor_tensor(out=z_sb[r][:], in0=x_sb[q][:, i, :], in1=bias_sb[:], op=ALU.add)
-                return
             for u in range(2):
                 c = slice(DS * u, DS * u + DS)
-                nc.vector.tensor_tensor(out=z_sb[r][:, c], in0=bias_ps[u][:], in1=x_sb[q][:, i, c], op=ALU.add)
+                if p0_on_gpsimd(r, u):
+                    nc.gpsimd.tensor_tensor(out=z_sb[r][:, c], in0=x_sb[q][:, i, c], in1=bias_sb[:, c], op=ALU.add)
+                else:
+                    nc.vector.tensor_tensor(out=z_sb[r][:, c], in0=bias_ps[u][:], in1=x_sb[q][:, i, c], op=ALU.add)
 
         def mm(r, u):
             q, i = divmod(r, ROWS)
@@ -221,6 +147,14 @@ def tile_tpru_pb_t_kernel(tc, a, vr, h, x2g, w_g, b_g, bg, out):
         def p1(r, u):
             c = slice(DS * u, DS * u + DS)
             nc.vector.tensor_tensor(out=z_sb[r][:, c], in0=acc_ps[(r, u)][:], in1=z_sb[r][:, c], op=ALU.add)
+
+        def sig(r):
+            if r == NT - 1:
+                for u in range(2):
+                    c = slice(DS * u, DS * u + DS)
+                    nc.scalar.activation(out=z_sb[r][:, c], in_=z_sb[r][:, c], func=ACT.Sigmoid)
+            else:
+                nc.scalar.activation(out=z_sb[r][:], in_=z_sb[r][:], func=ACT.Sigmoid)
 
         def d_open(r, s):
             q, i = divmod(r, ROWS)
@@ -259,6 +193,12 @@ def tile_tpru_pb_t_kernel(tc, a, vr, h, x2g, w_g, b_g, bg, out):
                     op=ALU.mult,
                 )
 
+        def p5(r, eng):
+            q, i = divmod(r, ROWS)
+            for s in range(S):
+                c = slice(DS * s, DS * s + DS)
+                eng.tensor_tensor(out=o_sb[r][:, c], in0=o_sb[r][:, c], in1=h_sb[q][:, i, c], op=ALU.add)
+
         def store(r):
             q, i = divmod(r, ROWS)
             nc.sync.dma_start(out=o_v[q][:, i, :], in_=o_sb[r][:])
@@ -266,50 +206,142 @@ def tile_tpru_pb_t_kernel(tc, a, vr, h, x2g, w_g, b_g, bg, out):
         def ok(r):
             return 0 <= r < NT
 
-        with tc.manual_schedule():
-            for r in range(-K0, NT + 3):
-                if r >= -ROWS and r % ROWS == 0 and r // ROWS + 3 < GROUPS:
-                    load_x(r // ROWS + 3)
-                if r >= -1 and r % ROWS == ROWS - 1 and (r + 9) // ROWS < GROUPS:
-                    load_h((r + 9) // ROWS)
-                    load_a((r + 9) // ROWS)
-                for u in range(2):
-                    if ok(r):
-                        p1(r, u)
-                    if ok(r + 1):
-                        mm(r + 1, u)
+        brow = const.tile([P, P], BF16, name="brow")
+        nc.vector.memset(brow[:], 0.0)
+        nc.sync.dma_start(out=brow[0:8, :], in_=b_g.rearrange("(j c) -> j c", c=P))
+        bg_b = const.tile([P, 1], BF16, name="bg_b")
+        nc.sync.dma_start(out=bg_b[:], in_=bg.partition_broadcast(P))
+
+        ident_b = const.tile([P, P], BF16, name="ident_b")
+        make_identity(nc, ident_b[:])
+        ident_f = const.tile([P, P], F32, name="ident_f")
+        make_identity(nc, ident_f[:])
+
+        wc = const.tile([P, 2, D], U32, name="wc", align_bytes=64)
+        ws = const.tile([P, 2, D], U8, name="ws", align_bytes=64)
+        vr_sb = const.tile([P, S, DS], BF16, name="vr_sb")
+        vrp_sb = const.tile([P, S, DS], BF16, name="vrp_sb")
+        bias_sb = const.tile([P, D], F32, name="bias_sb")
+        neg_i = const.tile([P, P], BF16, name="neg_i")
+
+        wtmp = tc.tile_pool(name="wtmp", bufs=1)
+        with wtmp as wt:
+            wraw = wt.tile([P, 8, D], BF16, name="wraw")
+            load_x(0)
+            nc.sync.dma_start(out=wraw[:, 0:2, :], in_=w_v[:, 0:2, :])
+            nc.sync.dma_start(out=wraw[:, 2:4, :], in_=w_v[:, 2:4, :])
+            nc.sync.dma_start(out=wraw[:, 4:6, :], in_=w_v[:, 4:6, :])
+            nc.sync.dma_start(out=wraw[:, 6:8, :], in_=w_v[:, 6:8, :])
+            load_h(0)
+            load_a(0)
+            load_x(1)
+            nc.sync.dma_start(out=vr_sb[:], in_=vr)
+            load_h(1)
+            load_a(1)
+            load_x(2)
+
+            b_t = psum.tile([P, P], BF16, name="b_t", tag="tp")
+            nc.tensor.transpose(b_t[:], brow[:], ident_b[:])
+            bg_f = const.tile([P, 1], F32, name="bg_f")
+            nc.vector.tensor_copy(out=bg_f[:], in_=bg_b[:])
+            bcol = const.tile([P, 8], F32, name="bcol")
+            nc.vector.tensor_scalar_add(out=bcol[:], in0=b_t[:, 0:8], scalar1=bg_f[:, 0:1])
+            brep = wt.tile([P, 8, P], F32, name="brep")
+            nc.vector.tensor_copy(out=brep[:], in_=bcol[:].unsqueeze(2).to_broadcast([P, 8, P]))
+            nc.vector.tensor_scalar_mul(out=neg_i[:], in0=ident_b[:], scalar1=-1.0)
+            bias_ps = []
+            for u in range(2):
+                bias_ps.append(psb.tile([P, DS], F32, name="bias%d" % u))
+            for j in range(8):
+                nc.tensor.transpose(bias_ps[j // 4][:, P * (j % 4) : P * (j % 4) + P], brep[:, j, :], ident_f[:])
+            for u in range(2):
+                nc.scalar.copy(out=bias_sb[:, DS * u : DS * u + DS], in_=bias_ps[u][:])
+
+            wg = wt.tile([P, 2 * D * 4], BF16, name="wg", align_bytes=64)
+            wg_f = wg[:].bitcast(F32).rearrange("p (g c u) -> p g c u", g=2, c=D, u=2)
+            wg_q = wg[:].rearrange("p (g x) -> p g x", g=2)
+
+            def w_copy(j, eng):
+                tpw = psum.tile([P, 4, P], F32, name="tpw", tag="tp")
+                wj = wraw[:, j, :].bitcast(F32)
+                for blk in range(4):
+                    nc.tensor.transpose(tpw[:, blk, :], wj[:, word_step(blk)], ident_f[:])
+                eng(
+                    out=wg_f[:, :, P * j : P * j + P, :],
+                    in_=tpw[:].rearrange("p (g u) r -> p g r u", g=2, u=2),
+                )
+
+            def w_quant(g, u):
+                nc.vector.quantize_mx(
+                    out=wc[:, g, DS * u : DS * u + DS].bitcast(FP8X4),
+                    scales=ws[:, g, DS * u : DS * u + DS],
+                    in_=wg_q[:, g, 4 * DS * u : 4 * DS * u + 4 * DS],
+                )
+
+            for r in range(4):
+                p0(r)
+            for j in range(8):
+                w_copy(j, nc.scalar.copy if j % 2 == 0 else nc.vector.tensor_copy)
+                if j == 4:
+                    w_quant(0, 0)
+                    w_quant(1, 0)
+            for r in range(4):
+                t_h(r)
+                c_h(r)
+                if r == 0:
+                    w_quant(0, 1)
+                    w_quant(1, 1)
+                if r % 2 == 1:
+                    quant(r - 1, 2)
+            t_a(0)
+            c_a(0)
+            nc.scalar.copy(
+                out=vrp_sb[:].rearrange("n s (t p) -> n s t p", t=4, p=P),
+                in_=vr_sb[:].rearrange("n s (p t) -> n s t p", t=4, p=P),
+            )
+            for r in range(4, 6):
+                p0(r)
+
+        late = ctx.enter_context(tc.tile_pool(name="late", bufs=3))
+
+        for r in range(-4, NT + 3):
+            if r >= -1 and r % ROWS == 0 and r // ROWS + 3 < GROUPS:
+                load_x(r // ROWS + 3)
+            if r >= -1 and r % ROWS == ROWS - 1 and (r + 9) // ROWS < GROUPS:
+                load_h((r + 9) // ROWS)
+                load_a((r + 9) // ROWS)
+            for u in range(2):
                 if ok(r):
-                    nc.scalar.activation(out=z_sb[r][:], in_=z_sb[r][:], func=ACT.Sigmoid)
-                if ok(r + 4):
-                    c_h(r + 4)
-                if ok(r - 1):
-                    for s in range(S):
-                        p4(r - 1, s)
-                        if r - 1 == NT - 1:
-                            c = slice(DS * s, DS * s + DS)
-                            nc.vector.tensor_tensor(
-                                out=o_sb[r - 1][:, c], in0=o_sb[r - 1][:, c], in1=h_sb[GROUPS - 1][:, ROWS - 1, c], op=ALU.add
-                            )
-                            nc.sync.dma_start(out=o_v[GROUPS - 1][:, ROWS - 1, c], in_=o_sb[r - 1][:, c])
-                if ok(r):
-                    for s in range(S):
-                        d_open(r, s)
-                    for s in range(S):
-                        d_close(r, s)
-                if (r + 2) % ROWS == 0 and ok(r + 2):
-                    c_a((r + 2) // ROWS)
-                if ok(r + 2) and not is_x(r + 2):
-                    nh_make(r + 2)
-                if ok(r + K0):
-                    p0(r + K0)
-                if ok(r + 2) and (r + 2) % 2 == 0:
-                    quant(r + 2)
-                if ok(r - 1) and r - 1 < NT - 1:
-                    q1, i1 = divmod(r - 1, ROWS)
-                    nc.gpsimd.tensor_tensor(out=o_sb[r - 1][:], in0=o_sb[r - 1][:], in1=h_sb[q1][:, i1, :], op=ALU.add)
-                if ok(r + TF):
-                    t_h(r + TF)
-                if (r + 3) % ROWS == 0 and ok(r + 3):
-                    t_a((r + 3) // ROWS)
-                if ok(r - 2) and r - 2 < NT - 1:
-                    store(r - 2)
+                    p1(r, u)
+                if ok(r + 1):
+                    mm(r + 1, u)
+            if ok(r + CH) and r + CH >= 4:
+                c_h(r + CH)
+            if ok(r):
+                sig(r)
+            if (r + CH) % ROWS == 3 and ROWS <= r + CH < NT:
+                quant(r + CH - 3, 4)
+            if ok(r - 1):
+                for s in range(S):
+                    p4(r - 1, s)
+            if ok(r - 1):
+                p5(r - 1, nc.vector if r - 1 >= NT - 1 else nc.gpsimd)
+            if ok(r):
+                for s in range(S):
+                    d_open(r, s)
+                for s in range(S):
+                    d_close(r, s)
+            if (r + 2) % ROWS == 0 and ROWS <= r + 2 < NT:
+                c_a((r + 2) // ROWS)
+            if ok(r + 2) and not is_x(r + 2):
+                nh_make(r + 2)
+            if ok(r + K0) and r + K0 >= 6:
+                p0(r + K0)
+            if r % 2 == 1:
+                for rr in (r + TF, r + TF + 1):
+                    if ok(rr) and rr >= 4:
+                        t_h(rr)
+            if (r + 3) % ROWS == 0 and ROWS <= r + 3 < NT:
+                t_a((r + 3) // ROWS)
+            if ok(r - 2) and r - 2 < NT:
+                store(r - 2)

@@ -17,9 +17,9 @@ DS = D // S
 ROWS = 4
 GROUPS = B // (P * ROWS)
 NT = GROUPS * ROWS
-K0 = 8
-TF = 7
-CH = 6
+K0 = 6
+TF = 5
+CH = 5
 
 FLOPS = 2 * B * D * D + 2 * B * N * D
 
@@ -33,8 +33,8 @@ def is_x(r):
     return r % 2 == 0
 
 
-def p0_on_gpsimd(r, u):
-    return r < 8 and r % 2 == 1 or r >= 8 and r % 4 == 1
+def p0_on_gpsimd(r):
+    return r%4==2
 
 
 def tile_tpru_pb_t_kernel(tc, a, vr, h, x2g, w_g, b_g, bg, out):
@@ -96,15 +96,15 @@ def tile_tpru_pb_t_kernel(tc, a, vr, h, x2g, w_g, b_g, bg, out):
                 in_=hg_sb[q][:, i0 : i0 + nt, :].rearrange("p i x -> p (i x)"),
             )
 
-        def nh_make(r):
+        def nh_make(r, g):
             q, i = divmod(r, ROWS)
-            nh_sb[r] = late.tile([P, 2, 4, P], F32, name="nh", tag="nh")
-            for g in range(2):
-                nc.scalar.mul(
-                    out=nh_sb[r][:, g, :, :],
-                    in_=hg_sb[q][:, i, 4 * P * g : 4 * P * g + 4 * P].rearrange("p (r t) -> p t r", r=P, t=4),
-                    mul=-1.0,
-                )
+            if g == 0:
+                nh_sb[r] = late.tile([P, 2, 4, P], F32, name="nh", tag="nh")
+            nc.scalar.mul(
+                out=nh_sb[r][:, g, :, :],
+                in_=hg_sb[q][:, i, 4 * P * g : 4 * P * g + 4 * P].rearrange("p (r t) -> p t r", r=P, t=4),
+                mul=-1.0,
+            )
 
         def t_a(q):
             ta_ps[q] = psum.tile([P, ROWS, P], F32, name="tpa", tag="tp")
@@ -118,15 +118,15 @@ def tile_tpru_pb_t_kernel(tc, a, vr, h, x2g, w_g, b_g, bg, out):
                 in_=ta_ps[q][:].rearrange("p i b -> p (i b)").bitcast(BF16).rearrange("p (i b s) -> p i s b", i=ROWS, b=P, s=S),
             )
 
-        def p0(r):
+        def p0(r, u, eng):
             q, i = divmod(r, ROWS)
-            z_sb[r] = work.tile([P, D], F32, name="z_t", tag="z", bufs=K0 + 3)
-            for u in range(2):
-                c = slice(DS * u, DS * u + DS)
-                if p0_on_gpsimd(r, u):
-                    nc.gpsimd.tensor_tensor(out=z_sb[r][:, c], in0=x_sb[q][:, i, c], in1=bias_sb[:, c], op=ALU.add)
-                else:
-                    nc.vector.tensor_tensor(out=z_sb[r][:, c], in0=bias_ps[u][:], in1=x_sb[q][:, i, c], op=ALU.add)
+            if u == 0:
+                z_sb[r] = work.tile([P, D], F32, name="z_t", tag="z", bufs=K0 + 3)
+            c = slice(DS * u, DS * u + DS)
+            if eng == 0:
+                nc.gpsimd.tensor_tensor(out=z_sb[r][:, c], in0=x_sb[q][:, i, c], in1=bias_sb[:, c], op=ALU.add)
+            else:
+                nc.vector.tensor_tensor(out=z_sb[r][:, c], in0=bias_ps[u][:], in1=x_sb[q][:, i, c], op=ALU.add)
 
         def mm(r, u):
             q, i = divmod(r, ROWS)
@@ -148,13 +148,9 @@ def tile_tpru_pb_t_kernel(tc, a, vr, h, x2g, w_g, b_g, bg, out):
             c = slice(DS * u, DS * u + DS)
             nc.vector.tensor_tensor(out=z_sb[r][:, c], in0=acc_ps[(r, u)][:], in1=z_sb[r][:, c], op=ALU.add)
 
-        def sig(r):
-            if r == NT - 1:
-                for u in range(2):
-                    c = slice(DS * u, DS * u + DS)
-                    nc.scalar.activation(out=z_sb[r][:, c], in_=z_sb[r][:, c], func=ACT.Sigmoid)
-            else:
-                nc.scalar.activation(out=z_sb[r][:], in_=z_sb[r][:], func=ACT.Sigmoid)
+        def sig(r, u):
+            c = slice(DS * u, DS * u + DS)
+            nc.scalar.activation(out=z_sb[r][:, c], in_=z_sb[r][:, c], func=ACT.Sigmoid)
 
         def d_open(r, s):
             q, i = divmod(r, ROWS)
@@ -193,11 +189,10 @@ def tile_tpru_pb_t_kernel(tc, a, vr, h, x2g, w_g, b_g, bg, out):
                     op=ALU.mult,
                 )
 
-        def p5(r, eng):
+        def p5(r, s, eng):
             q, i = divmod(r, ROWS)
-            for s in range(S):
-                c = slice(DS * s, DS * s + DS)
-                eng.tensor_tensor(out=o_sb[r][:, c], in0=o_sb[r][:, c], in1=h_sb[q][:, i, c], op=ALU.add)
+            c = slice(DS * s, DS * s + DS)
+            eng.tensor_tensor(out=o_sb[r][:, c], in0=o_sb[r][:, c], in1=h_sb[q][:, i, c], op=ALU.add)
 
         def store(r):
             q, i = divmod(r, ROWS)
@@ -227,15 +222,15 @@ def tile_tpru_pb_t_kernel(tc, a, vr, h, x2g, w_g, b_g, bg, out):
         wtmp = tc.tile_pool(name="wtmp", bufs=1)
         with wtmp as wt:
             wraw = wt.tile([P, 8, D], BF16, name="wraw")
-            load_x(0)
-            nc.sync.dma_start(out=wraw[:, 0:2, :], in_=w_v[:, 0:2, :])
-            nc.sync.dma_start(out=wraw[:, 2:4, :], in_=w_v[:, 2:4, :])
-            nc.sync.dma_start(out=wraw[:, 4:6, :], in_=w_v[:, 4:6, :])
-            nc.sync.dma_start(out=wraw[:, 6:8, :], in_=w_v[:, 6:8, :])
-            load_h(0)
+            for j in range(0, 8, 2):
+                nc.sync.dma_start(out=wraw[:, j : j + 2, :], in_=w_v[:, j : j + 2, :])
+            load_h(0, 0, 2)
+            load_x(0, 0, 2)
+            load_h(0, 2, 4)
+            load_x(0, 2, 4)
             load_a(0)
-            load_x(1)
             nc.sync.dma_start(out=vr_sb[:], in_=vr)
+            load_x(1)
             load_h(1)
             load_a(1)
             load_x(2)
@@ -254,18 +249,27 @@ def tile_tpru_pb_t_kernel(tc, a, vr, h, x2g, w_g, b_g, bg, out):
                 bias_ps.append(psb.tile([P, DS], F32, name="bias%d" % u))
             for j in range(8):
                 nc.tensor.transpose(bias_ps[j // 4][:, P * (j % 4) : P * (j % 4) + P], brep[:, j, :], ident_f[:])
-            for u in range(2):
-                nc.scalar.copy(out=bias_sb[:, DS * u : DS * u + DS], in_=bias_ps[u][:])
+
+            def bias_out():
+                for u in range(2):
+                    nc.scalar.copy(out=bias_sb[:, DS * u : DS * u + DS], in_=bias_ps[u][:])
 
             wg = wt.tile([P, 2 * D * 4], BF16, name="wg", align_bytes=64)
             wg_f = wg[:].bitcast(F32).rearrange("p (g c u) -> p g c u", g=2, c=D, u=2)
             wg_q = wg[:].rearrange("p (g x) -> p g x", g=2)
 
+            wperm = wt.tile([P, 8, 4, P], F32, name="wperm")
+
+            def w_perm(j):
+                nc.vector.tensor_copy(
+                    out=wperm[:, j, :, :].rearrange("p (g u) w -> p g u w", g=2, u=2),
+                    in_=wraw[:, j, :].bitcast(F32).rearrange("p (g w u) -> p g u w", g=2, w=P, u=2),
+                )
+
             def w_copy(j, eng):
                 tpw = psum.tile([P, 4, P], F32, name="tpw", tag="tp")
-                wj = wraw[:, j, :].bitcast(F32)
                 for blk in range(4):
-                    nc.tensor.transpose(tpw[:, blk, :], wj[:, word_step(blk)], ident_f[:])
+                    nc.tensor.transpose(tpw[:, blk, :], wperm[:, j, blk, :], ident_f[:])
                 eng(
                     out=wg_f[:, :, P * j : P * j + P, :],
                     in_=tpw[:].rearrange("p (g u) r -> p g r u", g=2, u=2),
@@ -278,70 +282,76 @@ def tile_tpru_pb_t_kernel(tc, a, vr, h, x2g, w_g, b_g, bg, out):
                     in_=wg_q[:, g, 4 * DS * u : 4 * DS * u + 4 * DS],
                 )
 
-            for r in range(4):
-                p0(r)
             for j in range(8):
-                w_copy(j, nc.scalar.copy if j % 2 == 0 else nc.vector.tensor_copy)
+                w_perm(j)
+            for j in range(8):
+                w_copy(j, nc.scalar.copy)
                 if j == 4:
                     w_quant(0, 0)
                     w_quant(1, 0)
-            for r in range(4):
-                t_h(r)
-                c_h(r)
-                if r == 0:
-                    w_quant(0, 1)
-                    w_quant(1, 1)
-                if r % 2 == 1:
-                    quant(r - 1, 2)
+            for u in range(2):
+                p0(0, u, 1)
+            t_h(0)
+            t_h(1)
+            c_h(0)
+            c_h(1)
+            bias_out()
+            w_quant(0, 1)
+            w_quant(1, 1)
+            quant(0, 2)
+            t_h(2)
+            c_h(2)
+            for u in range(2):
+                mm(0, u)
+            t_h(3)
+            c_h(3)
             t_a(0)
             c_a(0)
+            for r in range(1, 5):
+                for u in range(2):
+                    p0(r, u, 1 if r < 3 else 0)
             nc.scalar.copy(
                 out=vrp_sb[:].rearrange("n s (t p) -> n s t p", t=4, p=P),
                 in_=vr_sb[:].rearrange("n s (p t) -> n s t p", t=4, p=P),
             )
-            for r in range(4, 6):
-                p0(r)
 
         late = ctx.enter_context(tc.tile_pool(name="late", bufs=3))
 
-        for r in range(-4, NT + 3):
+        for r in range(-1, NT + 3):
             if r >= -1 and r % ROWS == 0 and r // ROWS + 3 < GROUPS:
                 load_x(r // ROWS + 3)
             if r >= -1 and r % ROWS == ROWS - 1 and (r + 9) // ROWS < GROUPS:
                 load_h((r + 9) // ROWS)
                 load_a((r + 9) // ROWS)
             for u in range(2):
+                if u == 1 and ok(r + CH) and r + CH >= 4:
+                    c_h(r + CH)
                 if ok(r):
                     p1(r, u)
-                if ok(r + 1):
+                if u == 1 and (r + CH) % ROWS == 3 and ROWS <= r + CH < NT:
+                    quant(r + CH - 3, 4)
+                if r == 0 and u == 1:
+                    quant(2, 2)
+                if ok(r - 1):
+                    p4(r - 1, u)
+                if ok(r):
+                    sig(r, u)
+                if u == 1 and (r + 2) % ROWS == 0 and ROWS <= r + 2 < NT:
+                    c_a((r + 2) // ROWS)
+                if ok(r + 2) and not is_x(r + 2):
+                    nh_make(r + 2, u)
+                if ok(r + 1) and r + 1 > 0:
                     mm(r + 1, u)
-            if ok(r + CH) and r + CH >= 4:
-                c_h(r + CH)
-            if ok(r):
-                sig(r)
-            if (r + CH) % ROWS == 3 and ROWS <= r + CH < NT:
-                quant(r + CH - 3, 4)
-            if ok(r - 1):
-                for s in range(S):
-                    p4(r - 1, s)
-            if ok(r - 1):
-                p5(r - 1, nc.vector if r - 1 >= NT - 1 else nc.gpsimd)
-            if ok(r):
-                for s in range(S):
-                    d_open(r, s)
-                for s in range(S):
-                    d_close(r, s)
-            if (r + 2) % ROWS == 0 and ROWS <= r + 2 < NT:
-                c_a((r + 2) // ROWS)
-            if ok(r + 2) and not is_x(r + 2):
-                nh_make(r + 2)
-            if ok(r + K0) and r + K0 >= 6:
-                p0(r + K0)
-            if r % 2 == 1:
-                for rr in (r + TF, r + TF + 1):
-                    if ok(rr) and rr >= 4:
-                        t_h(rr)
-            if (r + 3) % ROWS == 0 and ROWS <= r + 3 < NT:
-                t_a((r + 3) // ROWS)
+                if ok(r):
+                    d_open(r, u)
+                    d_close(r, u)
+                if r % 2 == 1 and ok(r + TF + u) and r + TF + u >= 4:
+                    t_h(r + TF + u)
+                if u == 1 and (r + 3) % ROWS == 0 and ROWS <= r + 3 < NT:
+                    t_a((r + 3) // ROWS)
+                if ok(r - 1):
+                    p5(r - 1, u, nc.vector if r - 1 >= NT - 1 else nc.gpsimd)
+                if ok(r + K0) and r + K0 >= 5:
+                    p0(r + K0, u, 0 if p0_on_gpsimd(r + K0) else 1)
             if ok(r - 2) and r - 2 < NT:
                 store(r - 2)

@@ -18,7 +18,7 @@ ROWS = 4
 GROUPS = B // (P * ROWS)
 NT = GROUPS * ROWS
 K0 = 6
-TF = 5
+TF = 6
 CH = 5
 
 FLOPS = 2 * B * D * D + 2 * B * N * D
@@ -34,7 +34,7 @@ def is_x(r):
 
 
 def p0_on_gpsimd(r):
-    return r%4==2
+    return r % 4 == 0
 
 
 def tile_tpru_pb_t_kernel(tc, a, vr, h, x2g, w_g, b_g, bg, out):
@@ -120,9 +120,11 @@ def tile_tpru_pb_t_kernel(tc, a, vr, h, x2g, w_g, b_g, bg, out):
 
         def p0(r, u, eng):
             q, i = divmod(r, ROWS)
-            if u == 0:
+            if u != 1:
                 z_sb[r] = work.tile([P, D], F32, name="z_t", tag="z", bufs=K0 + 3)
             c = slice(DS * u, DS * u + DS)
+            if u == 2:
+                c = slice(0, D)
             if eng == 0:
                 nc.gpsimd.tensor_tensor(out=z_sb[r][:, c], in0=x_sb[q][:, i, c], in1=bias_sb[:, c], op=ALU.add)
             else:
@@ -150,6 +152,8 @@ def tile_tpru_pb_t_kernel(tc, a, vr, h, x2g, w_g, b_g, bg, out):
 
         def sig(r, u):
             c = slice(DS * u, DS * u + DS)
+            if u == 2:
+                c = slice(0, D)
             nc.scalar.activation(out=z_sb[r][:, c], in_=z_sb[r][:, c], func=ACT.Sigmoid)
 
         def d_open(r, s):
@@ -192,6 +196,8 @@ def tile_tpru_pb_t_kernel(tc, a, vr, h, x2g, w_g, b_g, bg, out):
         def p5(r, s, eng):
             q, i = divmod(r, ROWS)
             c = slice(DS * s, DS * s + DS)
+            if s == 2:
+                c = slice(0, D)
             eng.tensor_tensor(out=o_sb[r][:, c], in0=o_sb[r][:, c], in1=h_sb[q][:, i, c], op=ALU.add)
 
         def store(r):
@@ -308,8 +314,11 @@ def tile_tpru_pb_t_kernel(tc, a, vr, h, x2g, w_g, b_g, bg, out):
             t_a(0)
             c_a(0)
             for r in range(1, 5):
-                for u in range(2):
-                    p0(r, u, 1 if r < 3 else 0)
+                if r < 3:
+                    p0(r, 0, 1)
+                    p0(r, 1, 1)
+                else:
+                    p0(r, 2, 0)
             nc.scalar.copy(
                 out=vrp_sb[:].rearrange("n s (t p) -> n s t p", t=4, p=P),
                 in_=vr_sb[:].rearrange("n s (p t) -> n s t p", t=4, p=P),
@@ -317,41 +326,58 @@ def tile_tpru_pb_t_kernel(tc, a, vr, h, x2g, w_g, b_g, bg, out):
 
         late = ctx.enter_context(tc.tile_pool(name="late", bufs=3))
 
-        for r in range(-1, NT + 3):
+        for r in range(-2, NT + 3):
             if r >= -1 and r % ROWS == 0 and r // ROWS + 3 < GROUPS:
                 load_x(r // ROWS + 3)
             if r >= -1 and r % ROWS == ROWS - 1 and (r + 9) // ROWS < GROUPS:
                 load_h((r + 9) // ROWS)
                 load_a((r + 9) // ROWS)
+            if ok(r + CH) and r + CH >= 4:
+                c_h(r + CH)
             for u in range(2):
-                if u == 1 and ok(r + CH) and r + CH >= 4:
-                    c_h(r + CH)
                 if ok(r):
                     p1(r, u)
-                if u == 1 and (r + CH) % ROWS == 3 and ROWS <= r + CH < NT:
-                    quant(r + CH - 3, 4)
-                if r == 0 and u == 1:
-                    quant(2, 2)
-                if ok(r - 1):
-                    p4(r - 1, u)
-                if ok(r):
-                    sig(r, u)
-                if u == 1 and (r + 2) % ROWS == 0 and ROWS <= r + 2 < NT:
-                    c_a((r + 2) // ROWS)
-                if ok(r + 2) and not is_x(r + 2):
-                    nh_make(r + 2, u)
                 if ok(r + 1) and r + 1 > 0:
                     mm(r + 1, u)
-                if ok(r):
-                    d_open(r, u)
-                    d_close(r, u)
-                if r % 2 == 1 and ok(r + TF + u) and r + TF + u >= 4:
-                    t_h(r + TF + u)
-                if u == 1 and (r + 3) % ROWS == 0 and ROWS <= r + 3 < NT:
-                    t_a((r + 3) // ROWS)
-                if ok(r - 1):
-                    p5(r - 1, u, nc.vector if r - 1 >= NT - 1 else nc.gpsimd)
-                if ok(r + K0) and r + K0 >= 5:
-                    p0(r + K0, u, 0 if p0_on_gpsimd(r + K0) else 1)
+            if r == 0:
+                quant(2, 2)
+            if (r + CH) % ROWS == 3 and ROWS <= r + CH < NT:
+                quant(r + CH - 3, 4)
+            if ok(r):
+                if r == NT - 1:
+                    sig(r, 0)
+                    sig(r, 1)
+                else:
+                    sig(r, 2)
+            if ok(r - 1):
+                for s in range(S):
+                    p4(r - 1, s)
+                if r - 1 == NT - 1:
+                    p5(r - 1, 0, nc.vector)
+                    p5(r - 1, 1, nc.vector)
+                else:
+                    p5(r - 1, 2, nc.gpsimd)
+            if ok(r):
+                for s in range(S):
+                    d_open(r, s)
+                for s in range(S):
+                    d_close(r, s)
+            if (r + 2) % ROWS == 0 and ROWS <= r + 2 < NT:
+                c_a((r + 2) // ROWS)
+            if ok(r + 2) and not is_x(r + 2):
+                nh_make(r + 2, 0)
+                nh_make(r + 2, 1)
+            if ok(r + K0) and r + K0 >= 5:
+                if p0_on_gpsimd(r + K0):
+                    p0(r + K0, 2, 0)
+                else:
+                    p0(r + K0, 0, 1)
+                    p0(r + K0, 1, 1)
+            if r % 2 == 0:
+                for rr in (r + TF, r + TF + 1):
+                    if ok(rr) and rr >= 4:
+                        t_h(rr)
+            if (r + 3) % ROWS == 0 and ROWS <= r + 3 < NT:
+                t_a((r + 3) // ROWS)
             if ok(r - 2) and r - 2 < NT:
                 store(r - 2)

@@ -72,7 +72,7 @@ def tile_tpru_pb_t_kernel(tc, a, vr, h, x2g, w_g, b_g, bg, out):
 
         def t_h(r):
             q, i = divmod(r, ROWS)
-            tp_ps[r] = psum.tile([P, 4, P], F32, name="tph", tag="tp")
+            tp_ps[r] = psum.tile([P, 4, P], F32, name="tph", tag="tp", bufs=3)
             hw = h_sb[q][:, i, :].bitcast(F32)
             for blk in range(4):
                 nc.tensor.transpose(tp_ps[r][:, blk, :], hw[:, word_step(blk)], ident_f[:])
@@ -107,7 +107,7 @@ def tile_tpru_pb_t_kernel(tc, a, vr, h, x2g, w_g, b_g, bg, out):
             )
 
         def t_a(q):
-            ta_ps[q] = psum.tile([P, ROWS, P], F32, name="tpa", tag="tp")
+            ta_ps[q] = psum.tile([P, ROWS, P], F32, name="tpa", tag="tp", bufs=3)
             for i in range(ROWS):
                 nc.tensor.transpose(ta_ps[q][:, i, :], a_sb[q][:, i, :].bitcast(F32), ident_f[:])
 
@@ -118,22 +118,20 @@ def tile_tpru_pb_t_kernel(tc, a, vr, h, x2g, w_g, b_g, bg, out):
                 in_=ta_ps[q][:].rearrange("p i b -> p (i b)").bitcast(BF16).rearrange("p (i b s) -> p i s b", i=ROWS, b=P, s=S),
             )
 
-        def p0(r, u, eng):
+        def p0(r, eng):
             q, i = divmod(r, ROWS)
-            if u != 1:
-                z_sb[r] = work.tile([P, D], F32, name="z_t", tag="z", bufs=K0 + 3)
-            c = slice(DS * u, DS * u + DS)
-            if u == 2:
-                c = slice(0, D)
+            z_sb[r] = work.tile([P, D], F32, name="z_t", tag="z", bufs=K0 + 3)
             if eng == 0:
-                nc.gpsimd.tensor_tensor(out=z_sb[r][:, c], in0=x_sb[q][:, i, c], in1=bias_sb[:, c], op=ALU.add)
+                nc.gpsimd.tensor_tensor(out=z_sb[r][:], in0=x_sb[q][:, i, :], in1=bias_sb[:], op=ALU.add)
             else:
-                nc.vector.tensor_tensor(out=z_sb[r][:, c], in0=bias_ps[u][:], in1=x_sb[q][:, i, c], op=ALU.add)
+                nc.vector.scalar_tensor_tensor(
+                    out=z_sb[r][:], in0=x_sb[q][:, i, :], scalar=bg_f[:, 0:1], in1=b_ps[:], op0=ALU.add, op1=ALU.add
+                )
 
         def mm(r, u):
             q, i = divmod(r, ROWS)
             c = slice(DS * u, DS * u + DS)
-            acc = psum.tile([P, DS], F32, name="acc", tag="h2g")
+            acc = psum.tile([P, DS], F32, name="acc", tag="h2g", bufs=2)
             for g in range(2):
                 nc.tensor.matmul_mx(
                     out=acc[:],
@@ -158,7 +156,7 @@ def tile_tpru_pb_t_kernel(tc, a, vr, h, x2g, w_g, b_g, bg, out):
 
         def d_open(r, s):
             q, i = divmod(r, ROWS)
-            hb = psum.tile([P, DS], F32, name="hb", tag="hh")
+            hb = psum.tile([P, DS], F32, name="hb", tag="hh", bufs=2)
             rhs = vr_sb if is_x(r) else vrp_sb
             nc.tensor.matmul(out=hb[:], lhsT=aT_sb[q][:, i, s, :], rhs=rhs[:, s, :], start=True, stop=False)
             hh_ps[(r, s)] = hb
@@ -213,6 +211,10 @@ def tile_tpru_pb_t_kernel(tc, a, vr, h, x2g, w_g, b_g, bg, out):
         bg_b = const.tile([P, 1], BF16, name="bg_b")
         nc.sync.dma_start(out=bg_b[:], in_=bg.partition_broadcast(P))
 
+        warm = const.tile([P, 1], F32, name="warm")
+        nc.vector.memset(warm[:], 0.0)
+        nc.scalar.activation(out=warm[:], in_=warm[:], func=ACT.Sigmoid)
+
         ident_b = const.tile([P, P], BF16, name="ident_b")
         make_identity(nc, ident_b[:])
         ident_f = const.tile([P, P], F32, name="ident_f")
@@ -241,24 +243,19 @@ def tile_tpru_pb_t_kernel(tc, a, vr, h, x2g, w_g, b_g, bg, out):
             load_a(1)
             load_x(2)
 
-            b_t = psum.tile([P, P], BF16, name="b_t", tag="tp")
+            b_t = psum.tile([P, P], BF16, name="b_t", tag="tp", bufs=3)
             nc.tensor.transpose(b_t[:], brow[:], ident_b[:])
             bg_f = const.tile([P, 1], F32, name="bg_f")
             nc.vector.tensor_copy(out=bg_f[:], in_=bg_b[:])
-            bcol = const.tile([P, 8], F32, name="bcol")
-            nc.vector.tensor_scalar_add(out=bcol[:], in0=b_t[:, 0:8], scalar1=bg_f[:, 0:1])
-            brep = wt.tile([P, 8, P], F32, name="brep")
-            nc.vector.tensor_copy(out=brep[:], in_=bcol[:].unsqueeze(2).to_broadcast([P, 8, P]))
+            bcol = const.tile([P, 8], BF16, name="bcol")
+            nc.vector.tensor_copy(out=bcol[:], in_=b_t[:, 0:8])
             nc.vector.tensor_scalar_mul(out=neg_i[:], in0=ident_b[:], scalar1=-1.0)
-            bias_ps = []
-            for u in range(2):
-                bias_ps.append(psb.tile([P, DS], F32, name="bias%d" % u))
+            b_ps = psb.tile([P, D], BF16, name="b_ps")
             for j in range(8):
-                nc.tensor.transpose(bias_ps[j // 4][:, P * (j % 4) : P * (j % 4) + P], brep[:, j, :], ident_f[:])
+                nc.tensor.transpose(b_ps[:, P * j : P * j + P], bcol[:, j : j + 1].to_broadcast([P, P]), ident_b[:])
 
             def bias_out():
-                for u in range(2):
-                    nc.scalar.copy(out=bias_sb[:, DS * u : DS * u + DS], in_=bias_ps[u][:])
+                nc.scalar.activation(out=bias_sb[:], in_=b_ps[:], func=ACT.Identity, bias=bg_f[:])
 
             wg = wt.tile([P, 2 * D * 4], BF16, name="wg", align_bytes=64)
             wg_f = wg[:].bitcast(F32).rearrange("p (g c u) -> p g c u", g=2, c=D, u=2)
@@ -273,7 +270,7 @@ def tile_tpru_pb_t_kernel(tc, a, vr, h, x2g, w_g, b_g, bg, out):
                 )
 
             def w_copy(j, eng):
-                tpw = psum.tile([P, 4, P], F32, name="tpw", tag="tp")
+                tpw = psum.tile([P, 4, P], F32, name="tpw", tag="tp", bufs=3)
                 for blk in range(4):
                     nc.tensor.transpose(tpw[:, blk, :], wperm[:, j, blk, :], ident_f[:])
                 eng(
@@ -295,8 +292,7 @@ def tile_tpru_pb_t_kernel(tc, a, vr, h, x2g, w_g, b_g, bg, out):
                 if j == 4:
                     w_quant(0, 0)
                     w_quant(1, 0)
-            for u in range(2):
-                p0(0, u, 1)
+            p0(0, 1)
             t_h(0)
             t_h(1)
             c_h(0)
@@ -314,11 +310,7 @@ def tile_tpru_pb_t_kernel(tc, a, vr, h, x2g, w_g, b_g, bg, out):
             t_a(0)
             c_a(0)
             for r in range(1, 5):
-                if r < 3:
-                    p0(r, 0, 1)
-                    p0(r, 1, 1)
-                else:
-                    p0(r, 2, 0)
+                p0(r, 1 if r < 3 else 0)
             nc.scalar.copy(
                 out=vrp_sb[:].rearrange("n s (t p) -> n s t p", t=4, p=P),
                 in_=vr_sb[:].rearrange("n s (p t) -> n s t p", t=4, p=P),
@@ -349,6 +341,11 @@ def tile_tpru_pb_t_kernel(tc, a, vr, h, x2g, w_g, b_g, bg, out):
                     sig(r, 1)
                 else:
                     sig(r, 2)
+            for rr in (r + TF,):
+                if ok(rr) and rr >= 4:
+                    t_h(rr)
+            if (r + 3) % ROWS == 0 and ROWS <= r + 3 < NT:
+                t_a((r + 3) // ROWS)
             if ok(r - 1):
                 for s in range(S):
                     p4(r - 1, s)
@@ -368,16 +365,8 @@ def tile_tpru_pb_t_kernel(tc, a, vr, h, x2g, w_g, b_g, bg, out):
                 nh_make(r + 2, 0)
                 nh_make(r + 2, 1)
             if ok(r + K0) and r + K0 >= 5:
-                if p0_on_gpsimd(r + K0):
-                    p0(r + K0, 2, 0)
-                else:
-                    p0(r + K0, 0, 1)
-                    p0(r + K0, 1, 1)
-            if r % 2 == 0:
-                for rr in (r + TF, r + TF + 1):
-                    if ok(rr) and rr >= 4:
-                        t_h(rr)
-            if (r + 3) % ROWS == 0 and ROWS <= r + 3 < NT:
-                t_a((r + 3) // ROWS)
+                p0(r + K0, 0 if p0_on_gpsimd(r + K0) else 1)
+
+
             if ok(r - 2) and r - 2 < NT:
                 store(r - 2)

@@ -17,7 +17,7 @@ DS = D // S
 ROWS = 4
 GROUPS = B // (P * ROWS)
 NT = GROUPS * ROWS
-K0 = 6
+K0 = 7
 TF = 6
 CH = 5
 
@@ -34,7 +34,7 @@ def is_x(r):
 
 
 def p0_on_gpsimd(r):
-    return r % 4 == 0
+    return r % 4 == 1
 
 
 def tile_tpru_pb_t_kernel(tc, a, vr, h, x2g, w_g, b_g, bg, out):
@@ -156,7 +156,7 @@ def tile_tpru_pb_t_kernel(tc, a, vr, h, x2g, w_g, b_g, bg, out):
 
         def d_open(r, s):
             q, i = divmod(r, ROWS)
-            hb = psum.tile([P, DS], F32, name="hb", tag="hh", bufs=2)
+            hb = psum.tile([P, DS], F32, name="hb", tag="tp" if r == NT - 1 else "hh", bufs=3 if r == NT - 1 else 2)
             rhs = vr_sb if is_x(r) else vrp_sb
             nc.tensor.matmul(out=hb[:], lhsT=aT_sb[q][:, i, s, :], rhs=rhs[:, s, :], start=True, stop=False)
             hh_ps[(r, s)] = hb
@@ -198,6 +198,11 @@ def tile_tpru_pb_t_kernel(tc, a, vr, h, x2g, w_g, b_g, bg, out):
                 c = slice(0, D)
             eng.tensor_tensor(out=o_sb[r][:, c], in0=o_sb[r][:, c], in1=h_sb[q][:, i, c], op=ALU.add)
 
+        def store_half(r, s):
+            q, i = divmod(r, ROWS)
+            c = slice(DS * s, DS * s + DS)
+            nc.sync.dma_start(out=o_v[q][:, i, c], in_=o_sb[r][:, c])
+
         def store(r):
             q, i = divmod(r, ROWS)
             nc.sync.dma_start(out=o_v[q][:, i, :], in_=o_sb[r][:])
@@ -230,8 +235,10 @@ def tile_tpru_pb_t_kernel(tc, a, vr, h, x2g, w_g, b_g, bg, out):
         wtmp = tc.tile_pool(name="wtmp", bufs=1)
         with wtmp as wt:
             wraw = wt.tile([P, 8, D], BF16, name="wraw")
-            for j in range(0, 8, 2):
-                nc.sync.dma_start(out=wraw[:, j : j + 2, :], in_=w_v[:, j : j + 2, :])
+            nc.sync.dma_start(out=wraw[:, 0:2, :], in_=w_v[:, 0:2, :])
+            nc.sync.dma_start(out=wraw[:, 2:4, :], in_=w_v[:, 2:4, :])
+            nc.sync.dma_start(out=wraw[:, 4:6, :], in_=w_v[:, 4:6, :])
+            nc.sync.dma_start(out=wraw[:, 6:8, :], in_=w_v[:, 6:8, :])
             load_h(0, 0, 2)
             load_x(0, 0, 2)
             load_h(0, 2, 4)
@@ -287,12 +294,12 @@ def tile_tpru_pb_t_kernel(tc, a, vr, h, x2g, w_g, b_g, bg, out):
 
             for j in range(8):
                 w_perm(j)
+            p0(0, 1)
             for j in range(8):
                 w_copy(j, nc.scalar.copy)
                 if j == 4:
                     w_quant(0, 0)
                     w_quant(1, 0)
-            p0(0, 1)
             t_h(0)
             t_h(1)
             c_h(0)
@@ -309,8 +316,14 @@ def tile_tpru_pb_t_kernel(tc, a, vr, h, x2g, w_g, b_g, bg, out):
             c_h(3)
             t_a(0)
             c_a(0)
-            for r in range(1, 5):
-                p0(r, 1 if r < 3 else 0)
+            p0(1, 1)
+            p0(3, 0)
+            p0(4, 0)
+            p0(5, 0)
+            p0(6, 0)
+            for s in range(S):
+                d_open(0, s)
+                d_close(0, s)
             nc.scalar.copy(
                 out=vrp_sb[:].rearrange("n s (t p) -> n s t p", t=4, p=P),
                 in_=vr_sb[:].rearrange("n s (p t) -> n s t p", t=4, p=P),
@@ -318,13 +331,13 @@ def tile_tpru_pb_t_kernel(tc, a, vr, h, x2g, w_g, b_g, bg, out):
 
         late = ctx.enter_context(tc.tile_pool(name="late", bufs=3))
 
-        for r in range(-2, NT + 3):
+        for r in range(-1, NT + 3):
             if r >= -1 and r % ROWS == 0 and r // ROWS + 3 < GROUPS:
                 load_x(r // ROWS + 3)
             if r >= -1 and r % ROWS == ROWS - 1 and (r + 9) // ROWS < GROUPS:
                 load_h((r + 9) // ROWS)
                 load_a((r + 9) // ROWS)
-            if ok(r + CH) and r + CH >= 4:
+            if r > 0 and ok(r + CH):
                 c_h(r + CH)
             for u in range(2):
                 if ok(r):
@@ -332,16 +345,15 @@ def tile_tpru_pb_t_kernel(tc, a, vr, h, x2g, w_g, b_g, bg, out):
                 if ok(r + 1) and r + 1 > 0:
                     mm(r + 1, u)
             if r == 0:
+                p0(2, 1)
                 quant(2, 2)
-            if (r + CH) % ROWS == 3 and ROWS <= r + CH < NT:
-                quant(r + CH - 3, 4)
             if ok(r):
                 if r == NT - 1:
                     sig(r, 0)
                     sig(r, 1)
                 else:
                     sig(r, 2)
-            for rr in (r + TF,):
+            for rr in ((4, 5, 6) if r == 0 else (r + TF,) if r > 0 else ()):
                 if ok(rr) and rr >= 4:
                     t_h(rr)
             if (r + 3) % ROWS == 0 and ROWS <= r + 3 < NT:
@@ -349,24 +361,34 @@ def tile_tpru_pb_t_kernel(tc, a, vr, h, x2g, w_g, b_g, bg, out):
             if ok(r - 1):
                 for s in range(S):
                     p4(r - 1, s)
+            if (r + CH) % ROWS == 3 and ROWS <= r + CH < NT:
+                quant(r + CH - 3, 4)
+            if ok(r - 1):
                 if r - 1 == NT - 1:
+                    for s in range(S):
+                        p5(r - 1, s, nc.vector)
+                        store_half(r - 1, s)
+                elif False:
                     p5(r - 1, 0, nc.vector)
                     p5(r - 1, 1, nc.vector)
                 else:
                     p5(r - 1, 2, nc.gpsimd)
-            if ok(r):
+            if ok(r) and r > 0:
                 for s in range(S):
                     d_open(r, s)
                 for s in range(S):
                     d_close(r, s)
+            if r == 0:
+                c_h(4)
+                c_h(5)
             if (r + 2) % ROWS == 0 and ROWS <= r + 2 < NT:
                 c_a((r + 2) // ROWS)
             if ok(r + 2) and not is_x(r + 2):
                 nh_make(r + 2, 0)
                 nh_make(r + 2, 1)
-            if ok(r + K0) and r + K0 >= 5:
+            if ok(r + K0) and r + K0 >= 7:
                 p0(r + K0, 0 if p0_on_gpsimd(r + K0) else 1)
 
 
-            if ok(r - 2) and r - 2 < NT:
+            if ok(r - 2) and r - 2 < NT - 1:
                 store(r - 2)

@@ -264,9 +264,9 @@ def tile_tpru_pb_t_kernel(tc, a, vr, h, x2g, w_g, b_g, bg, out):
             def bias_out():
                 nc.scalar.activation(out=bias_sb[:], in_=b_ps[:], func=ACT.Identity, bias=bg_f[:])
 
-            wg = wt.tile([P, 2 * D * 4], BF16, name="wg", align_bytes=64)
-            wg_f = wg[:].bitcast(F32).rearrange("p (g c u) -> p g c u", g=2, c=D, u=2)
-            wg_q = wg[:].rearrange("p (g x) -> p g x", g=2)
+            wg = []
+            for u in range(2):
+                wg.append(wt.tile([P, 2, DS * 4], BF16, name="wg%d" % u, align_bytes=64))
 
             wperm = wt.tile([P, 8, 4, P], F32, name="wperm")
 
@@ -281,7 +281,7 @@ def tile_tpru_pb_t_kernel(tc, a, vr, h, x2g, w_g, b_g, bg, out):
                 for blk in range(4):
                     nc.tensor.transpose(tpw[:, blk, :], wperm[:, j, blk, :], ident_f[:])
                 eng(
-                    out=wg_f[:, :, P * j : P * j + P, :],
+                    out=wg[j // 4][:].bitcast(F32).rearrange("p g (c u) -> p g c u", u=2)[:, :, P * (j % 4) : P * (j % 4) + P, :],
                     in_=tpw[:].rearrange("p (g u) r -> p g r u", g=2, u=2),
                 )
 
@@ -289,33 +289,38 @@ def tile_tpru_pb_t_kernel(tc, a, vr, h, x2g, w_g, b_g, bg, out):
                 nc.vector.quantize_mx(
                     out=wc[:, g, DS * u : DS * u + DS].bitcast(FP8X4),
                     scales=ws[:, g, DS * u : DS * u + DS],
-                    in_=wg_q[:, g, 4 * DS * u : 4 * DS * u + 4 * DS],
+                    in_=wg[u][:, g, :],
                 )
 
             for j in range(8):
                 w_perm(j)
+            w_copy(0, nc.scalar.copy)
+            w_copy(1, nc.scalar.copy)
+            w_copy(2, nc.scalar.copy)
+            w_copy(3, nc.scalar.copy)
+            w_copy(4, nc.scalar.copy)
+            w_copy(5, nc.scalar.copy)
+            w_copy(6, nc.scalar.copy)
+            w_copy(7, nc.scalar.copy)
+            w_quant(0, 0)
+            w_quant(1, 0)
             p0(0, 1)
-            for j in range(8):
-                w_copy(j, nc.scalar.copy)
-                if j == 4:
-                    w_quant(0, 0)
-                    w_quant(1, 0)
             t_h(0)
             t_h(1)
             c_h(0)
             c_h(1)
-            bias_out()
             w_quant(0, 1)
             w_quant(1, 1)
+            bias_out()
             quant(0, 2)
-            t_h(2)
-            c_h(2)
-            for u in range(2):
-                mm(0, u)
-            t_h(3)
-            c_h(3)
             t_a(0)
             c_a(0)
+            mm(0, 0)
+            mm(0, 1)
+            t_h(2)
+            c_h(2)
+            t_h(3)
+            c_h(3)
             p0(1, 1)
             p0(3, 0)
             p0(4, 0)
@@ -353,11 +358,13 @@ def tile_tpru_pb_t_kernel(tc, a, vr, h, x2g, w_g, b_g, bg, out):
                     sig(r, 1)
                 else:
                     sig(r, 2)
-            for rr in ((4, 5, 6) if r == 0 else (r + TF,) if r > 0 else ()):
-                if ok(rr) and rr >= 4:
+            if r == 0:
+                for rr in (4, 5, 6):
                     t_h(rr)
-            if (r + 3) % ROWS == 0 and ROWS <= r + 3 < NT:
-                t_a((r + 3) // ROWS)
+            if ok(r + TF) and r + TF >= 4 and r > 0 and r % 2 == 0:
+                t_h(r + TF)
+            if ok(r + TF) and r + TF >= 4 and r > 0 and r % 2 == 1:
+                t_h(r + TF)
             if ok(r - 1):
                 for s in range(S):
                     p4(r - 1, s)
@@ -388,7 +395,7 @@ def tile_tpru_pb_t_kernel(tc, a, vr, h, x2g, w_g, b_g, bg, out):
                 nh_make(r + 2, 1)
             if ok(r + K0) and r + K0 >= 7:
                 p0(r + K0, 0 if p0_on_gpsimd(r + K0) else 1)
-
-
+            if (r + 3) % ROWS == 0 and ROWS <= r + 3 < NT:
+                t_a((r + 3) // ROWS)
             if ok(r - 2) and r - 2 < NT - 1:
                 store(r - 2)

@@ -118,9 +118,17 @@ def tile_tpru_pb_t_kernel(tc, a, vr, h, x2g, w_g, b_g, bg, out):
                 in_=ta_ps[q][:].rearrange("p i b -> p (i b)").bitcast(BF16).rearrange("p (i b s) -> p i s b", i=ROWS, b=P, s=S),
             )
 
+        def z_new(r):
+            z_sb[r] = work.tile([P, D], F32, name="z_t", tag="z", bufs=K0 + 3)
+
+        def z_mark(r):
+            z_new(r)
+            nc.vector.memset(z_sb[r][:, 0:1], 0.0)
+
         def p0(r, eng):
             q, i = divmod(r, ROWS)
-            z_sb[r] = work.tile([P, D], F32, name="z_t", tag="z", bufs=K0 + 3)
+            if r not in z_sb:
+                z_new(r)
             if eng == 0:
                 nc.gpsimd.tensor_tensor(out=z_sb[r][:], in0=x_sb[q][:, i, :], in1=bias_sb[:], op=ALU.add)
             else:
@@ -313,6 +321,7 @@ def tile_tpru_pb_t_kernel(tc, a, vr, h, x2g, w_g, b_g, bg, out):
             w_quant(1, 1)
             bias_out()
             quant(0, 2)
+            z_mark(3)
             t_a(0)
             c_a(0)
             mm(0, 0)
@@ -324,8 +333,6 @@ def tile_tpru_pb_t_kernel(tc, a, vr, h, x2g, w_g, b_g, bg, out):
             p0(1, 1)
             p0(3, 0)
             p0(4, 0)
-            p0(5, 0)
-            p0(6, 0)
             for s in range(S):
                 d_open(0, s)
                 d_close(0, s)
@@ -352,6 +359,10 @@ def tile_tpru_pb_t_kernel(tc, a, vr, h, x2g, w_g, b_g, bg, out):
             if r == 0:
                 p0(2, 1)
                 quant(2, 2)
+                z_mark(5)
+                p0(5, 0)
+                p0(6, 0)
+
             if ok(r):
                 if r == NT - 1:
                     sig(r, 0)
@@ -370,6 +381,9 @@ def tile_tpru_pb_t_kernel(tc, a, vr, h, x2g, w_g, b_g, bg, out):
                     p4(r - 1, s)
             if (r + CH) % ROWS == 3 and ROWS <= r + CH < NT:
                 quant(r + CH - 3, 4)
+            if ok(r + K0) and r + K0 >= 7 and p0_on_gpsimd(r + K0):
+                z_mark(r + K0)
+                p0(r + K0, 0)
             if ok(r - 1):
                 if r - 1 == NT - 1:
                     for s in range(S):
@@ -393,8 +407,8 @@ def tile_tpru_pb_t_kernel(tc, a, vr, h, x2g, w_g, b_g, bg, out):
             if ok(r + 2) and not is_x(r + 2):
                 nh_make(r + 2, 0)
                 nh_make(r + 2, 1)
-            if ok(r + K0) and r + K0 >= 7:
-                p0(r + K0, 0 if p0_on_gpsimd(r + K0) else 1)
+            if ok(r + K0) and r + K0 >= 7 and not p0_on_gpsimd(r + K0):
+                p0(r + K0, 1)
             if (r + 3) % ROWS == 0 and ROWS <= r + 3 < NT:
                 t_a((r + 3) // ROWS)
             if ok(r - 2) and r - 2 < NT - 1:

@@ -17,7 +17,7 @@ DS = D // S
 ROWS = 4
 GROUPS = B // (P * ROWS)
 NT = GROUPS * ROWS
-K0 = 7
+K0 = 6
 TF = 6
 CH = 5
 
@@ -34,7 +34,7 @@ def is_x(r):
 
 
 def p0_on_gpsimd(r):
-    return r % 4 == 1
+    return r % 4 == 0
 
 
 def tile_tpru_pb_t_kernel(tc, a, vr, h, x2g, w_g, b_g, bg, out):
@@ -332,7 +332,6 @@ def tile_tpru_pb_t_kernel(tc, a, vr, h, x2g, w_g, b_g, bg, out):
             c_h(3)
             p0(1, 1)
             p0(3, 0)
-            p0(4, 0)
             for s in range(S):
                 d_open(0, s)
                 d_close(0, s)
@@ -359,9 +358,9 @@ def tile_tpru_pb_t_kernel(tc, a, vr, h, x2g, w_g, b_g, bg, out):
             if r == 0:
                 p0(2, 1)
                 quant(2, 2)
-                z_mark(5)
+                z_mark(4)
+                p0(4, 0)
                 p0(5, 0)
-                p0(6, 0)
 
             if ok(r):
                 if r == NT - 1:
@@ -376,22 +375,24 @@ def tile_tpru_pb_t_kernel(tc, a, vr, h, x2g, w_g, b_g, bg, out):
                 t_h(r + TF)
             if ok(r + TF) and r + TF >= 4 and r > 0 and r % 2 == 1:
                 t_h(r + TF)
-            if ok(r - 1):
-                for s in range(S):
+            for s in range(S):
+                if ok(r - 1):
                     p4(r - 1, s)
-            if (r + CH) % ROWS == 3 and ROWS <= r + CH < NT:
-                quant(r + CH - 3, 4)
-            if ok(r + K0) and r + K0 >= 7 and p0_on_gpsimd(r + K0):
+                if (r + CH) % ROWS == 3 and ROWS <= r + CH < NT and s == (1 if ok(r + K0) else 0):
+                    quant(r + CH - 3, 4)
+            if ok(r + K0) and r + K0 >= 6 and p0_on_gpsimd(r + K0):
                 z_mark(r + K0)
                 p0(r + K0, 0)
             if ok(r - 1):
                 if r - 1 == NT - 1:
+                    p5(r - 2, 1, nc.vector)
+                    store_half(r - 2, 1)
                     for s in range(S):
                         p5(r - 1, s, nc.vector)
                         store_half(r - 1, s)
-                elif False:
-                    p5(r - 1, 0, nc.vector)
-                    p5(r - 1, 1, nc.vector)
+                elif r - 1 == NT - 2:
+                    p5(r - 1, 0, nc.gpsimd)
+                    store_half(r - 1, 0)
                 else:
                     p5(r - 1, 2, nc.gpsimd)
             if ok(r) and r > 0:
@@ -407,9 +408,9 @@ def tile_tpru_pb_t_kernel(tc, a, vr, h, x2g, w_g, b_g, bg, out):
             if ok(r + 2) and not is_x(r + 2):
                 nh_make(r + 2, 0)
                 nh_make(r + 2, 1)
-            if ok(r + K0) and r + K0 >= 7 and not p0_on_gpsimd(r + K0):
+            if ok(r + K0) and r + K0 >= 6 and not p0_on_gpsimd(r + K0):
                 p0(r + K0, 1)
             if (r + 3) % ROWS == 0 and ROWS <= r + 3 < NT:
                 t_a((r + 3) // ROWS)
-            if ok(r - 2) and r - 2 < NT - 1:
+            if ok(r - 2) and r - 2 < NT - 2:
                 store(r - 2)

@@ -56,6 +56,8 @@ def tile_tpru_pb_t_kernel(tc, a, vr, h, x2g, w_g, b_g, bg, out):
         h_sb, x_sb, a_sb, aT_sb, tp_ps, ta_ps = {}, {}, {}, {}, {}, {}
         hg_sb, hc_sb, hs_sb, nh_sb, acc_ps, hh_ps, z_sb, o_sb = {}, {}, {}, {}, {}, {}, {}, {}
 
+        xt_ps, xbt_sb, xb_ps = {}, {}, {}
+
         def load_x(q, lo=0, hi=ROWS):
             if lo == 0:
                 x_sb[q] = ld.tile([P, ROWS, D], BF16, name="x_t", tag="x")
@@ -133,8 +135,36 @@ def tile_tpru_pb_t_kernel(tc, a, vr, h, x2g, w_g, b_g, bg, out):
                 nc.gpsimd.tensor_tensor(out=z_sb[r][:], in0=x_sb[q][:, i, :], in1=bias_sb[:], op=ALU.add)
             else:
                 nc.vector.scalar_tensor_tensor(
-                    out=z_sb[r][:], in0=x_sb[q][:, i, :], scalar=bg_f[:, 0:1], in1=b_ps[:], op0=ALU.add, op1=ALU.add
+                    out=z_sb[r][:], in0=x_sb[q][:, i, :], scalar=bg_f[:, 0:1], in1=b_ps[:].bitcast(BF16), op0=ALU.add, op1=ALU.add
                 )
+
+        def xt_a(r):
+            q, i = divmod(r, ROWS)
+            xt = psum.tile([P, 4, P], F32, name="xt", tag="tp", bufs=3)
+            xw = x_sb[q][:, i, :].bitcast(F32)
+            for blk in range(4):
+                nc.tensor.transpose(xt[:, blk, :], xw[:, P * blk : P * blk + P], ident_f[:])
+            xt_ps[r] = xt
+
+        def xt_o(r):
+            xbt_sb[r] = late.tile([P, 8, P], F32, name="xbt", tag="xbt", bufs=2)
+            w = xt_ps[r][:].rearrange("p k b -> p (k b)").bitcast(BF16).rearrange("p (k b e) -> p k e b", k=4, b=P, e=2)
+            for m in range(8):
+                nc.scalar.activation(out=xbt_sb[r][:, m, :], in_=w[:, m // 2, m % 2, :], func=ACT.Identity, bias=bcw[:, m : m + 1])
+
+        def xt_b(r, u):
+            xb = psum.tile([P, DS], F32, name="xb", tag="tp", bufs=3)
+            for m in range(4):
+                nc.tensor.transpose(xb[:, P * m : P * m + P], xbt_sb[r][:, 4 * u + m, :], ident_f[:])
+            xb_ps[(r, u)] = xb
+
+        def xt_z(r, u):
+            if u == 0:
+                z_new(r)
+            nc.scalar.copy(
+                out=z_sb[r][:, DS * u : DS * u + DS].rearrange("b (k p e) -> b k p e", k=2, p=P, e=2),
+                in_=xb_ps[(r, u)][:].rearrange("b (k e p) -> b k p e", k=2, e=2, p=P),
+            )
 
         def mm(r, u):
             q, i = divmod(r, ROWS)
@@ -218,20 +248,20 @@ def tile_tpru_pb_t_kernel(tc, a, vr, h, x2g, w_g, b_g, bg, out):
         def ok(r):
             return 0 <= r < NT
 
-        brow = const.tile([P, P], BF16, name="brow")
+        brow = const.tile([P, 2 * P], BF16, name="brow")
         nc.vector.memset(brow[:], 0.0)
-        nc.sync.dma_start(out=brow[0:8, :], in_=b_g.rearrange("(j c) -> j c", c=P))
+        nc.sync.dma_start(out=brow[0:4, :], in_=b_g.rearrange("(j c) -> j c", c=2 * P))
         bg_b = const.tile([P, 1], BF16, name="bg_b")
         nc.sync.dma_start(out=bg_b[:], in_=bg.partition_broadcast(P))
 
+        ident_f = const.tile([P, P], F32, name="ident_f")
+        make_identity(nc, ident_f[:])
         warm = const.tile([P, 1], F32, name="warm")
         nc.vector.memset(warm[:], 0.0)
         nc.scalar.activation(out=warm[:], in_=warm[:], func=ACT.Sigmoid)
 
         ident_b = const.tile([P, P], BF16, name="ident_b")
         make_identity(nc, ident_b[:])
-        ident_f = const.tile([P, P], F32, name="ident_f")
-        make_identity(nc, ident_f[:])
 
         wc = const.tile([P, 2, D], U32, name="wc", align_bytes=64)
         ws = const.tile([P, 2, D], U8, name="ws", align_bytes=64)
@@ -258,19 +288,21 @@ def tile_tpru_pb_t_kernel(tc, a, vr, h, x2g, w_g, b_g, bg, out):
             load_a(1)
             load_x(2)
 
-            b_t = psum.tile([P, P], BF16, name="b_t", tag="tp", bufs=3)
-            nc.tensor.transpose(b_t[:], brow[:], ident_b[:])
+            b_t = psum.tile([P, P], F32, name="b_t", tag="tp", bufs=3)
+            nc.tensor.transpose(b_t[:], brow[:].bitcast(F32), ident_f[:])
+            bcol = const.tile([P, 4], F32, name="bcol")
+            nc.vector.tensor_copy(out=bcol[:], in_=b_t[:, 0:4])
             bg_f = const.tile([P, 1], F32, name="bg_f")
             nc.vector.tensor_copy(out=bg_f[:], in_=bg_b[:])
-            bcol = const.tile([P, 8], BF16, name="bcol")
-            nc.vector.tensor_copy(out=bcol[:], in_=b_t[:, 0:8])
+            bcw = const.tile([P, 8], F32, name="bcw")
+            nc.vector.tensor_scalar_add(out=bcw[:], in0=b_t[:].bitcast(BF16)[:, 0:8], scalar1=bg_f[:, 0:1])
             nc.vector.tensor_scalar_mul(out=neg_i[:], in0=ident_b[:], scalar1=-1.0)
-            b_ps = psb.tile([P, D], BF16, name="b_ps")
-            for j in range(8):
-                nc.tensor.transpose(b_ps[:, P * j : P * j + P], bcol[:, j : j + 1].to_broadcast([P, P]), ident_b[:])
+            b_ps = psb.tile([P, DS], F32, name="b_ps")
+            for j in range(4):
+                nc.tensor.transpose(b_ps[:, P * j : P * j + P], bcol[:, j : j + 1].to_broadcast([P, P]), ident_f[:])
 
             def bias_out():
-                nc.scalar.activation(out=bias_sb[:], in_=b_ps[:], func=ACT.Identity, bias=bg_f[:])
+                nc.scalar.activation(out=bias_sb[:], in_=b_ps[:].bitcast(BF16), func=ACT.Identity, bias=bg_f[:])
 
             wg = []
             for u in range(2):
@@ -375,6 +407,12 @@ def tile_tpru_pb_t_kernel(tc, a, vr, h, x2g, w_g, b_g, bg, out):
                 t_h(r + TF)
             if ok(r + TF) and r + TF >= 4 and r > 0 and r % 2 == 1:
                 t_h(r + TF)
+            if r + 8 in (11, 19, 27):
+                xt_a(r + 8)
+            if r + 7 in (11, 19, 27):
+                xt_b(r + 7, 0)
+            if r + 6 in (11, 19, 27):
+                xt_b(r + 6, 1)
             for s in range(S):
                 if ok(r - 1):
                     p4(r - 1, s)
@@ -383,6 +421,8 @@ def tile_tpru_pb_t_kernel(tc, a, vr, h, x2g, w_g, b_g, bg, out):
             if ok(r + K0) and r + K0 >= 6 and p0_on_gpsimd(r + K0):
                 z_mark(r + K0)
                 p0(r + K0, 0)
+            if ok(r - 2) and r - 2 < NT - 2:
+                store(r - 2)
             if ok(r - 1):
                 if r - 1 == NT - 1:
                     p5(r - 2, 1, nc.vector)
@@ -408,9 +448,13 @@ def tile_tpru_pb_t_kernel(tc, a, vr, h, x2g, w_g, b_g, bg, out):
             if ok(r + 2) and not is_x(r + 2):
                 nh_make(r + 2, 0)
                 nh_make(r + 2, 1)
-            if ok(r + K0) and r + K0 >= 6 and not p0_on_gpsimd(r + K0):
+            if r + 8 in (11, 19, 27):
+                xt_o(r + 8)
+            if r + 7 in (11, 19, 27):
+                xt_z(r + 7, 0)
+            if r + 6 in (11, 19, 27):
+                xt_z(r + 6, 1)
+            if ok(r + K0) and r + K0 >= 6 and not p0_on_gpsimd(r + K0) and r + K0 not in (11, 19, 27):
                 p0(r + K0, 1)
             if (r + 3) % ROWS == 0 and ROWS <= r + 3 < NT:
                 t_a((r + 3) // ROWS)
-            if ok(r - 2) and r - 2 < NT - 2:
-                store(r - 2)

from contextlib import ExitStack

import concourse.mybir as mybir
from concourse.masks import make_identity

F32 = mybir.dt.float32
BF16 = mybir.dt.bfloat16
U32 = mybir.dt.uint32
U8 = mybir.dt.uint8
FP8X4 = mybir.dt.float8_e4m3fn_x4
ALU = mybir.AluOpType
ACT = mybir.ActivationFunctionType

P = 128
B, D, S, N = 4096, 1024, 2, 128
DS = D // S
ROWS = 4
GROUPS = B // (P * ROWS)
NT = GROUPS * ROWS
K0 = 6
TF = 6
CH = 5

FLOPS = 2 * B * D * D + 2 * B * N * D


def word_step(blk):
    g, u = divmod(blk, 2)
    return slice(256 * g + u, 256 * g + 256, 2)


def is_x(r):
    return r % 2 == 0


def p0_on_gpsimd(r):
    return r % 4 == 0


def tile_tpru_pb_t_kernel(tc, a, vr, h, x2g, w_g, b_g, bg, out):
    nc = tc.nc
    h_v = h.rearrange("(q p i) k -> q p i k", p=P, i=ROWS)
    x_v = x2g.rearrange("(q p i) k -> q p i k", p=P, i=ROWS)
    a_v = a.rearrange("(q p i) n s -> q p i (n s)", p=P, i=ROWS)
    o_v = out.rearrange("(q p i) k -> q p i k", p=P, i=ROWS)
    w_v = w_g.rearrange("(j p) k -> p j k", p=P)

    with ExitStack() as ctx:
        ctx.enter_context(tc.manual_schedule())
        const = ctx.enter_context(tc.tile_pool(name="const", bufs=1))
        ld = ctx.enter_context(tc.tile_pool(name="ld", bufs=3))
        work = ctx.enter_context(tc.tile_pool(name="work", bufs=2))
        psum = ctx.enter_context(tc.psum_pool(name="psum", bufs=2))
        psb = ctx.enter_context(tc.psum_pool(name="psb", bufs=1))

        h_sb, x_sb, a_sb, aT_sb, tp_ps, ta_ps = {}, {}, {}, {}, {}, {}
        hg_sb, hc_sb, hs_sb, nh_sb, acc_ps, hh_ps, z_sb, o_sb = {}, {}, {}, {}, {}, {}, {}, {}

        xt_ps, xbt_sb, xb_ps = {}, {}, {}

        def load_x(q, lo=0, hi=ROWS):
            if lo == 0:
                x_sb[q] = ld.tile([P, ROWS, D], BF16, name="x_t", tag="x")
            nc.sync.dma_start(out=x_sb[q][:, lo:hi, :], in_=x_v[q][:, lo:hi, :])

        def load_h(q, lo=0, hi=ROWS):
            if lo == 0:
                h_sb[q] = ld.tile([P, ROWS, D], BF16, name="h_t", tag="h", bufs=4)
            nc.sync.dma_start(out=h_sb[q][:, lo:hi, :], in_=h_v[q][:, lo:hi, :])

        def load_a(q):
            a_sb[q] = ld.tile([P, ROWS, 2 * N], BF16, name="a_t", tag="a")
            nc.sync.dma_start(out=a_sb[q][:], in_=a_v[q])

        def t_h(r):
            q, i = divmod(r, ROWS)
            tp_ps[r] = psum.tile([P, 4, P], F32, name="tph", tag="tp", bufs=3)
            hw = h_sb[q][:, i, :].bitcast(F32)
            for blk in range(4):
                nc.tensor.transpose(tp_ps[r][:, blk, :], hw[:, word_step(blk)], ident_f[:])

        def c_h(r):
            q, i = divmod(r, ROWS)
            if i == 0:
                hg_sb[q] = work.tile([P, ROWS, D], BF16, name="hg", tag="hg", align_bytes=64)
                hc_sb[q] = work.tile([P, ROWS, 2, P], U32, name="hc", tag="hc", align_bytes=64)
                hs_sb[q] = work.tile([P, ROWS, 2, P], U8, name="hs", tag="hs", align_bytes=64)
            nc.scalar.copy(
                out=hg_sb[q][:, i, :].bitcast(F32).rearrange("p (g r u) -> p g r u", g=2, r=P, u=2),
                in_=tp_ps[r][:].rearrange("p (g u) r -> p g r u", g=2, u=2),
            )

        def quant(r0, nt):
            q, i0 = divmod(r0, ROWS)
            nc.vector.quantize_mx(
                out=hc_sb[q][:, i0 : i0 + nt, :, :].rearrange("p i g r -> p (i g r)").bitcast(FP8X4),
                scales=hs_sb[q][:, i0 : i0 + nt, :, :].rearrange("p i g r -> p (i g r)"),
                in_=hg_sb[q][:, i0 : i0 + nt, :].rearrange("p i x -> p (i x)"),
            )

        def nh_make(r, g):
            q, i = divmod(r, ROWS)
            if g == 0:
                nh_sb[r] = late.tile([P, 2, 4, P], F32, name="nh", tag="nh")
            nc.scalar.mul(
                out=nh_sb[r][:, g, :, :],
                in_=hg_sb[q][:, i, 4 * P * g : 4 * P * g + 4 * P].rearrange("p (r t) -> p t r", r=P, t=4),
                mul=-1.0,
            )

        def t_a(q):
            ta_ps[q] = psum.tile([P, ROWS, P], F32, name="tpa", tag="tp", bufs=3)
            for i in range(ROWS):
                nc.tensor.transpose(ta_ps[q][:, i, :], a_sb[q][:, i, :].bitcast(F32), ident_f[:])

        def c_a(q):
            aT_sb[q] = work.tile([P, ROWS, S, P], BF16, name="aT", tag="aT")
            nc.scalar.copy(
                out=aT_sb[q][:],
                in_=ta_ps[q][:].rearrange("p i b -> p (i b)").bitcast(BF16).rearrange("p (i b s) -> p i s b", i=ROWS, b=P, s=S),
            )

        def z_new(r):
            z_sb[r] = work.tile([P, D], F32, name="z_t", tag="z", bufs=K0 + 3)

        def z_mark(r):
            z_new(r)
            nc.vector.memset(z_sb[r][:, 0:1], 0.0)

        def p0(r, eng):
            q, i = divmod(r, ROWS)
            if r not in z_sb:
                z_new(r)
            if eng == 0:
                nc.gpsimd.tensor_tensor(out=z_sb[r][:], in0=x_sb[q][:, i, :], in1=bias_sb[:], op=ALU.add)
            else:
                nc.vector.scalar_tensor_tensor(
                    out=z_sb[r][:], in0=x_sb[q][:, i, :], scalar=bg_f[:, 0:1], in1=b_ps[:].bitcast(BF16), op0=ALU.add, op1=ALU.add
                )

        def xt_a(r):
            q, i = divmod(r, ROWS)
            xt = psum.tile([P, 4, P], F32, name="xt", tag="tp", bufs=3)
            xw = x_sb[q][:, i, :].bitcast(F32)
            for blk in range(4):
                nc.tensor.transpose(xt[:, blk, :], xw[:, P * blk : P * blk + P], ident_f[:])
            xt_ps[r] = xt

        def xt_o(r):
            xbt_sb[r] = late.tile([P, 8, P], F32, name="xbt", tag="xbt", bufs=2)
            w = xt_ps[r][:].rearrange("p k b -> p (k b)").bitcast(BF16).rearrange("p (k b e) -> p k e b", k=4, b=P, e=2)
            for m in range(8):
                nc.scalar.activation(out=xbt_sb[r][:, m, :], in_=w[:, m // 2, m % 2, :], func=ACT.Identity, bias=bcw[:, m : m + 1])

        def xt_b(r, u):
            xb = psum.tile([P, DS], F32, name="xb", tag="tp", bufs=3)
            for m in range(4):
                nc.tensor.transpose(xb[:, P * m : P * m + P], xbt_sb[r][:, 4 * u + m, :], ident_f[:])
            xb_ps[(r, u)] = xb

        def xt_z(r, u):
            if u == 0:
                z_new(r)
            nc.scalar.copy(
                out=z_sb[r][:, DS * u : DS * u + DS].rearrange("b (k p e) -> b k p e", k=2, p=P, e=2),
                in_=xb_ps[(r, u)][:].rearrange("b (k e p) -> b k p e", k=2, e=2, p=P),
            )

        def mm(r, u):
            q, i = divmod(r, ROWS)
            c = slice(DS * u, DS * u + DS)
            acc = psum.tile([P, DS], F32, name="acc", tag="h2g", bufs=2)
            for g in range(2):
                nc.tensor.matmul_mx(
                    out=acc[:],
                    lhsT=hc_sb[q][:, i, g, :].bitcast(FP8X4),
                    lhsT_scale=hs_sb[q][:, i, g, :],
                    rhs=wc[:, g, c].bitcast(FP8X4),
                    rhs_scale=ws[:, g, c],
                    start=(g == 0),
                    stop=(g == 1),
                )
            acc_ps[(r, u)] = acc

        def p1(r, u):
            c = slice(DS * u, DS * u + DS)
            nc.vector.tensor_tensor(out=z_sb[r][:, c], in0=acc_ps[(r, u)][:], in1=z_sb[r][:, c], op=ALU.add)

        def sig(r, u):
            c = slice(DS * u, DS * u + DS)
            if u == 2:
                c = slice(0, D)
            nc.scalar.activation(out=z_sb[r][:, c], in_=z_sb[r][:, c], func=ACT.Sigmoid)

        def d_open(r, s):
            q, i = divmod(r, ROWS)
            hb = psum.tile([P, DS], F32, name="hb", tag="tp" if r == NT - 1 else "hh", bufs=3 if r == NT - 1 else 2)
            rhs = vr_sb if is_x(r) else vrp_sb
            nc.tensor.matmul(out=hb[:], lhsT=aT_sb[q][:, i, s, :], rhs=rhs[:, s, :], start=True, stop=False)
            hh_ps[(r, s)] = hb

        def d_close(r, s):
            q, i = divmod(r, ROWS)
            hb = hh_ps[(r, s)]
            if is_x(r):
                nc.tensor.matmul(out=hb[:], lhsT=neg_i[:], rhs=h_sb[q][:, i, DS * s : DS * s + DS], start=False, stop=True)
                return
            for t in range(4):
                nc.tensor.matmul(
                    out=hb[:, P * t : P * t + P],
                    lhsT=nh_sb[r][:, s, t, :],
                    rhs=ident_f[:],
                    start=False,
                    stop=(t == 3),
                    is_transpose=True,
                )

        def p4(r, s):
            c = slice(DS * s, DS * s + DS)
            if s == 0:
                o_sb[r] = late.tile([P, D], F32, name="o_t", tag="o", bufs=6)
            if is_x(r):
                nc.vector.tensor_tensor(out=o_sb[r][:, c], in0=hh_ps[(r, s)][:], in1=z_sb[r][:, c], op=ALU.mult)
            else:
                nc.vector.tensor_tensor(
                    out=o_sb[r][:, c].rearrange("r (p t) -> r p t", p=P, t=4),
                    in0=hh_ps[(r, s)][:].rearrange("r (t p) -> r p t", p=P, t=4),
                    in1=z_sb[r][:, c].rearrange("r (p t) -> r p t", p=P, t=4),
                    op=ALU.mult,
                )

        def p5(r, s, eng):
            q, i = divmod(r, ROWS)
            c = slice(DS * s, DS * s + DS)
            if s == 2:
                c = slice(0, D)
            eng.tensor_tensor(out=o_sb[r][:, c], in0=o_sb[r][:, c], in1=h_sb[q][:, i, c], op=ALU.add)

        def store_half(r, s):
            q, i = divmod(r, ROWS)
            c = slice(DS * s, DS * s + DS)
            nc.sync.dma_start(out=o_v[q][:, i, c], in_=o_sb[r][:, c])

        def store(r):
            q, i = divmod(r, ROWS)
            nc.sync.dma_start(out=o_v[q][:, i, :], in_=o_sb[r][:])

        def ok(r):
            return 0 <= r < NT

        brow = const.tile([P, 2 * P], BF16, name="brow")
        nc.vector.memset(brow[:], 0.0)
        nc.sync.dma_start(out=brow[0:4, :], in_=b_g.rearrange("(j c) -> j c", c=2 * P))
        bg_b = const.tile([P, 1], BF16, name="bg_b")
        nc.sync.dma_start(out=bg_b[:], in_=bg.partition_broadcast(P))

        ident_f = const.tile([P, P], F32, name="ident_f")
        make_identity(nc, ident_f[:])
        warm = const.tile([P, 1], F32, name="warm")
        nc.vector.memset(warm[:], 0.0)
        nc.scalar.activation(out=warm[:], in_=warm[:], func=ACT.Sigmoid)

        ident_b = const.tile([P, P], BF16, name="ident_b")
        make_identity(nc, ident_b[:])

        wc = const.tile([P, 2, D], U32, name="wc", align_bytes=64)
        ws = const.tile([P, 2, D], U8, name="ws", align_bytes=64)
        vr_sb = const.tile([P, S, DS], BF16, name="vr_sb")
        vrp_sb = const.tile([P, S, DS], BF16, name="vrp_sb")
        bias_sb = const.tile([P, D], F32, name="bias_sb")
        neg_i = const.tile([P, P], BF16, name="neg_i")

        wtmp = tc.tile_pool(name="wtmp", bufs=1)
        with wtmp as wt:
            wraw = wt.tile([P, 8, D], BF16, name="wraw")
            nc.sync.dma_start(out=wraw[:, 0:2, :], in_=w_v[:, 0:2, :])
            nc.sync.dma_start(out=wraw[:, 2:4, :], in_=w_v[:, 2:4, :])
            nc.sync.dma_start(out=wraw[:, 4:6, :], in_=w_v[:, 4:6, :])
            nc.sync.dma_start(out=wraw[:, 6:8, :], in_=w_v[:, 6:8, :])
            load_h(0, 0, 2)
            load_x(0, 0, 2)
            load_h(0, 2, 4)
            load_x(0, 2, 4)
            load_a(0)
            nc.sync.dma_start(out=vr_sb[:], in_=vr)
            load_x(1)
            load_h(1)
            load_a(1)
            load_x(2)

            b_t = psum.tile([P, P], F32, name="b_t", tag="tp", bufs=3)
            nc.tensor.transpose(b_t[:], brow[:].bitcast(F32), ident_f[:])
            bcol = const.tile([P, 4], F32, name="bcol")
            nc.vector.tensor_copy(out=bcol[:], in_=b_t[:, 0:4])
            bg_f = const.tile([P, 1], F32, name="bg_f")
            nc.vector.tensor_copy(out=bg_f[:], in_=bg_b[:])
            bcw = const.tile([P, 8], F32, name="bcw")
            nc.vector.tensor_scalar_add(out=bcw[:], in0=b_t[:].bitcast(BF16)[:, 0:8], scalar1=bg_f[:, 0:1])
            nc.vector.tensor_scalar_mul(out=neg_i[:], in0=ident_b[:], scalar1=-1.0)
            b_ps = psb.tile([P, DS], F32, name="b_ps")
            for j in range(4):
                nc.tensor.transpose(b_ps[:, P * j : P * j + P], bcol[:, j : j + 1].to_broadcast([P, P]), ident_f[:])

            def bias_out():
                nc.scalar.activation(out=bias_sb[:], in_=b_ps[:].bitcast(BF16), func=ACT.Identity, bias=bg_f[:])

            wg = []
            for u in range(2):
                wg.append(wt.tile([P, 2, DS * 4], BF16, name="wg%d" % u, align_bytes=64))

            wperm = wt.tile([P, 8, 4, P], F32, name="wperm")

            def w_perm(j):
                nc.vector.tensor_copy(
                    out=wperm[:, j, :, :].rearrange("p (g u) w -> p g u w", g=2, u=2),
                    in_=wraw[:, j, :].bitcast(F32).rearrange("p (g w u) -> p g u w", g=2, w=P, u=2),
                )

            def w_copy(j, eng):
                tpw = psum.tile([P, 4, P], F32, name="tpw", tag="tp", bufs=3)
                for blk in range(4):
                    nc.tensor.transpose(tpw[:, blk, :], wperm[:, j, blk, :], ident_f[:])
                eng(
                    out=wg[j // 4][:].bitcast(F32).rearrange("p g (c u) -> p g c u", u=2)[:, :, P * (j % 4) : P * (j % 4) + P, :],
                    in_=tpw[:].rearrange("p (g u) r -> p g r u", g=2, u=2),
                )

            def w_quant(g, u):
                nc.vector.quantize_mx(
                    out=wc[:, g, DS * u : DS * u + DS].bitcast(FP8X4),
                    scales=ws[:, g, DS * u : DS * u + DS],
                    in_=wg[u][:, g, :],
                )

            for j in range(8):
                w_perm(j)
            w_copy(0, nc.scalar.copy)
            w_copy(1, nc.scalar.copy)
            w_copy(2, nc.scalar.copy)
            w_copy(3, nc.scalar.copy)
            w_copy(4, nc.scalar.copy)
            w_copy(5, nc.scalar.copy)
            w_copy(6, nc.scalar.copy)
            w_copy(7, nc.scalar.copy)
            w_quant(0, 0)
            w_quant(1, 0)
            p0(0, 1)
            t_h(0)
            t_h(1)
            c_h(0)
            c_h(1)
            w_quant(0, 1)
            w_quant(1, 1)
            bias_out()
            quant(0, 2)
            z_mark(3)
            t_a(0)
            c_a(0)
            mm(0, 0)
            mm(0, 1)
            t_h(2)
            c_h(2)
            t_h(3)
            c_h(3)
            p0(1, 1)
            p0(3, 0)
            for s in range(S):
                d_open(0, s)
                d_close(0, s)
            nc.scalar.copy(
                out=vrp_sb[:].rearrange("n s (t p) -> n s t p", t=4, p=P),
                in_=vr_sb[:].rearrange("n s (p t) -> n s t p", t=4, p=P),
            )

        late = ctx.enter_context(tc.tile_pool(name="late", bufs=3))

        for r in range(-1, NT + 3):
            if r >= -1 and r % ROWS == 0 and r // ROWS + 3 < GROUPS:
                load_x(r // ROWS + 3)
            if r >= -1 and r % ROWS == ROWS - 1 and (r + 9) // ROWS < GROUPS:
                load_h((r + 9) // ROWS)
                load_a((r + 9) // ROWS)
            if r > 0 and ok(r + CH):
                c_h(r + CH)
            for u in range(2):
                if ok(r):
                    p1(r, u)
                if ok(r + 1) and r + 1 > 0:
                    mm(r + 1, u)
            if r == 0:
                p0(2, 1)
                quant(2, 2)
                z_mark(4)
                p0(4, 0)
                p0(5, 0)

            if ok(r):
                if r == NT - 1:
                    sig(r, 0)
                    sig(r, 1)
                else:
                    sig(r, 2)
            if r == 0:
                for rr in (4, 5, 6):
                    t_h(rr)
            if ok(r + TF) and r + TF >= 4 and r > 0 and r % 2 == 0:
                t_h(r + TF)
            if ok(r + TF) and r + TF >= 4 and r > 0 and r % 2 == 1:
                t_h(r + TF)
            if r + 8 in (11, 19, 27):
                xt_a(r + 8)
            if r + 7 in (11, 19, 27):
                xt_b(r + 7, 0)
            if r + 6 in (11, 19, 27):
                xt_b(r + 6, 1)
            for s in range(S):
                if ok(r - 1):
                    p4(r - 1, s)
                if (r + CH) % ROWS == 3 and ROWS <= r + CH < NT and s == (1 if ok(r + K0) else 0):
                    quant(r + CH - 3, 4)
            if ok(r + K0) and r + K0 >= 6 and p0_on_gpsimd(r + K0):
                z_mark(r + K0)
                p0(r + K0, 0)
            if ok(r - 2) and r - 2 < NT - 2:
                store(r - 2)
            if ok(r - 1):
                if r - 1 == NT - 1:
                    p5(r - 2, 1, nc.vector)
                    store_half(r - 2, 1)
                    for s in range(S):
                        p5(r - 1, s, nc.vector)
                        store_half(r - 1, s)
                elif r - 1 == NT - 2:
                    p5(r - 1, 0, nc.gpsimd)
                    store_half(r - 1, 0)
                else:
                    p5(r - 1, 2, nc.gpsimd)
            if ok(r) and r > 0:
                for s in range(S):
                    d_open(r, s)
                for s in range(S):
                    d_close(r, s)
            if r == 0:
                c_h(4)
                c_h(5)
            if (r + 2) % ROWS == 0 and ROWS <= r + 2 < NT:
                c_a((r + 2) // ROWS)
            if ok(r + 2) and not is_x(r + 2):
                nh_make(r + 2, 0)
                nh_make(r + 2, 1)
            if r + 8 in (11, 19, 27):
                xt_o(r + 8)
            if r + 7 in (11, 19, 27):
                xt_z(r + 7, 0)
            if r + 6 in (11, 19, 27):
                xt_z(r + 6, 1)
            if ok(r + K0) and r + K0 >= 6 and not p0_on_gpsimd(r + K0) and r + K0 not in (11, 19, 27):
                p0(r + K0, 1)
            if (r + 3) % ROWS == 0 and ROWS <= r + 3 < NT:
                t_a((r + 3) // ROWS)
